import numpy as np
import ml_dtypes


def mxq(x, axis, fmt="e4m3"):
    dtype, down = {"e4m3": (ml_dtypes.float8_e4m3fn, 7), "e5m2": (ml_dtypes.float8_e5m2, 14)}[fmt]
    v = np.moveaxis(np.asarray(x, np.float32).astype(ml_dtypes.bfloat16).astype(np.float64), axis, -1)
    blocks = v.reshape(v.shape[:-1] + (-1, 32))
    amax = np.abs(blocks).max(-1, keepdims=True)
    byte = np.maximum(np.where(amax > 0, np.frexp(amax)[1] - 1 + 127, 0) - down, 1)
    scale = np.exp2(byte - 127.0)
    codes = (blocks / scale).astype(np.float32).astype(dtype).astype(np.float64)
    return np.moveaxis((codes * scale).reshape(v.shape), -1, axis)


WIDE = False


def mx_kscale(k):
    if not WIDE:
        return np.ones(k)
    levels = np.array([10, -10, 5, -5, 0])
    a = np.random.permutation(np.resize(levels, k // 512 * 4)).reshape(k // 512, 4)
    idx = np.arange(k)
    return np.exp2(a[idx // 512, idx % 128 // 32])


BF16 = ml_dtypes.bfloat16


def bf(x):
    return np.asarray(x, np.float32).astype(BF16)


def f64(x):
    return np.asarray(x).astype(np.float64)


B, I, O, G, P = 1024, 512, 512, 5, 3
GRID_RANGE = (-1.0, 1.0)
L = G + P


def make_grid():
    h = (GRID_RANGE[1] - GRID_RANGE[0]) / G
    n = G + 2 * P + 1
    return np.linspace(GRID_RANGE[0] - P * h, GRID_RANGE[1] + P * h, n)


def b_spline(x, grid, k):
    x = x[..., None]
    g = grid[None, None, :]
    basis = ((x >= g[..., :-1]) & (x < g[..., 1:])).astype(np.float64)
    for p in range(1, k + 1):
        left_denom = g[..., p:-1] - g[..., :-(p + 1)]
        right_denom = g[..., p + 1:] - g[..., 1:-p]
        left_denom = np.where(left_denom > 0, left_denom, np.ones_like(left_denom))
        right_denom = np.where(right_denom > 0, right_denom, np.ones_like(right_denom))
        left = (x - g[..., :-(p + 1)]) / left_denom * basis[..., :-1]
        right = (g[..., p + 1:] - x) / right_denom * basis[..., 1:]
        basis = left + right
    return basis


def setup_inputs():
    s = mx_kscale(I)
    s = s / s.max()
    return {"x": bf(np.random.uniform(-1.0, 1.0, (B, I)) * s),
            "base_weight": bf(np.random.uniform(-1.0, 1.0, (O, I)) * 3.0 / np.sqrt(I) / s),
            "spline_weight": bf(np.random.standard_normal((O, I, L)) * 1.5 / np.sqrt(I))}


def reference(x, base_weight, spline_weight):
    x = f64(x)
    grid = make_grid()
    scale_base, scale_spline = 1.0, 1.0
    base_out = mxq(x, 1, "e4m3") @ mxq(f64(base_weight), 1, "e4m3").T
    basis = b_spline(x, grid, P)
    spline_out = mxq(basis.reshape(B, I * L), 1, "e4m3") @ mxq(f64(spline_weight).reshape(O, I * L), 1, "e4m3").T
    return scale_base * base_out + scale_spline * spline_out

@@ -1,0 +1,175 @@
+import math
+
+import concourse.mybir as mybir
+from concourse.masks import make_identity
+
+F32 = mybir.dt.float32
+BF16 = mybir.dt.bfloat16
+U32 = mybir.dt.uint32
+U8 = mybir.dt.uint8
+FP8X4 = mybir.dt.float8_e4m3fn_x4
+ACT = mybir.ActivationFunctionType
+ALU = mybir.AluOpType
+
+P = 128
+B, I, O, L = 1024, 512, 512, 8
+FLOPS = 2 * B * O * (I + I * L)
+
+CH = 4
+NB = B // P // CH
+N = NB * P * 4
+S3 = 1.0 / math.sqrt(3.0)
+KNOT = (-0.6, -0.2, 0.2, 0.6)
+
+
+def tile_kanlayer_kernel(tc, x, base_weight, spline_weight, out):
+    nc = tc.nc
+    with tc.tile_pool(name="keep", bufs=1) as keep, tc.tile_pool(name="wave", bufs=2) as wave, tc.tile_pool(
+        name="half", bufs=1
+    ) as half, tc.tile_pool(name="grp", bufs=2) as grp, tc.tile_pool(name="code", bufs=2) as code, tc.tile_pool(
+        name="res", bufs=3
+    ) as res, tc.psum_pool(name="pt", bufs=2) as pt, tc.psum_pool(name="pw", bufs=3) as pw, tc.psum_pool(
+        name="pa", bufs=3
+    ) as pa:
+        ident = keep.tile([P, P], F32)
+        make_identity(nc, ident[:])
+
+        x_raw = keep.tile([P, CH * NB, I], BF16)
+        x_rows = x.rearrange("(n p) i -> p n i", p=P)
+        bw_raw = keep.tile([P, O // P, I], BF16)
+        sw_raw = [keep.tile([P, I * L], BF16, name="sw_raw%d" % m) for m in range(O // P)]
+        sw_rows = spline_weight.rearrange("(m p) i l -> m p (i l)", p=P)
+        nc.sync.dma_start(out=x_raw[:, 0:4, :], in_=x_rows[:, 0:4, :])
+        nc.sync.dma_start(out=sw_raw[0][:], in_=sw_rows[0])
+        nc.sync.dma_start(out=x_raw[:, 4:8, :], in_=x_rows[:, 4:8, :])
+        nc.sync.dma_start(out=sw_raw[1][:], in_=sw_rows[1])
+        nc.sync.dma_start(out=bw_raw[:], in_=base_weight.rearrange("(m p) i -> p m i", p=P))
+        nc.sync.dma_start(out=sw_raw[2][:], in_=sw_rows[2])
+        nc.sync.dma_start(out=sw_raw[3][:], in_=sw_rows[3])
+
+        xg = keep.tile([P, CH, N], BF16, align_bytes=64)
+        x_codes = keep.tile([P, CH, N // 4], U32, align_bytes=64)
+        x_scales = keep.tile([P, CH, N // 4], U8, align_bytes=64)
+        bwg = keep.tile([P, 2, N], BF16, align_bytes=64)
+        bw_codes = keep.tile([P, O], U32, align_bytes=64)
+        bw_scales = keep.tile([P, O], U8, align_bytes=64)
+        w_codes = keep.tile([P, L, O], U32, align_bytes=64)
+        w_scales = keep.tile([P, L, O], U8, align_bytes=64)
+
+        def turn_rows(raw_words, dst):
+            bank = pt.tile([P, NB, 2, P], F32, name="bank")
+            for n in range(NB):
+                for u in range(2):
+                    nc.tensor.transpose(bank[:, n, u, :], raw_words[:, n, u * P : (u + 1) * P], ident[:])
+            nc.scalar.copy(
+                out=dst.bitcast(F32).rearrange("p (n b u) -> p n b u", n=NB, u=2),
+                in_=bank[:].rearrange("p n u b -> p n b u"),
+            )
+
+        xw = x_raw[:].bitcast(F32)
+        for c in range(CH):
+            turn_rows(xw[:, c * NB : (c + 1) * NB, :], xg[:, c, :])
+
+        def quantise(src, codes, scales):
+            nc.vector.quantize_mx(out=codes.bitcast(FP8X4), scales=scales, in_=src)
+
+        def weights(m):
+            words = sw_raw[m][:].bitcast(F32).rearrange("p (u q e j) -> p u e j q", u=2, q=P, e=2, j=4)
+            g = grp.tile([P, L, P * 4], BF16, align_bytes=64, name="g")
+            for j in range(4):
+                bank = pw.tile([P, 4, P], F32, name="wbank")
+                for u in range(2):
+                    for e in range(2):
+                        nc.tensor.transpose(bank[:, 2 * u + e, :], words[:, u, e, j, :], ident[:])
+                nc.scalar.copy(
+                    out=g[:, 2 * j : 2 * j + 2, :].rearrange("p s (o t) -> p s o t", t=4),
+                    in_=bank[:].bitcast(BF16).rearrange("p t (o s) -> p s o t", s=2),
+                )
+            for l in range(L):
+                quantise(g[:, l, :], w_codes[:, l, m * P : (m + 1) * P], w_scales[:, l, m * P : (m + 1) * P])
+
+        def base_weights():
+            bww = bw_raw[:].bitcast(F32)
+            for h in range(2):
+                turn_rows(bww[:, h * NB : (h + 1) * NB, :], bwg[:, h, :])
+            quantise(bwg[:].rearrange("p h n -> p (h n)"), bw_codes[:], bw_scales[:])
+
+        def basis(c):
+            xc = xg[:, c, :]
+            quantise(xc, x_codes[:, c, :], x_scales[:, c, :])
+            mask = half.tile([P, 4, N], BF16, name="mask")
+            for r in range(4):
+                nc.vector.tensor_scalar(
+                    out=mask[:, r, :], in0=xc, scalar1=KNOT[r], scalar2=0.5,
+                    op0=(ALU.is_lt if r < 2 else ALU.is_ge), op1=ALU.subtract,
+                )
+            zs, ks = [], []
+            for w in range(2):
+                z = wave.tile([P, N], F32, name="z%d" % w)
+                q = wave.tile([P, N], F32, name="q%d" % w)
+                k = wave.tile([P, N], F32, name="k%d" % w)
+                nc.scalar.activation(out=z[:], in_=xc, func=ACT.Abs, bias=-0.5 - w, scale=2.5)
+                nc.scalar.activation(out=z[:], in_=z[:], func=ACT.Abs, bias=-2.0, scale=1.0)
+                nc.scalar.activation(out=q[:], in_=z[:], func=ACT.Square, bias=-S3, scale=S3)
+                nc.vector.scalar_tensor_tensor(out=q[:], in0=z[:], scalar=1.0, in1=q[:], op0=ALU.subtract, op1=ALU.mult)
+                nc.scalar.activation(out=k[:], in_=q[:], func=ACT.Abs, scale=0.5)
+                nc.vector.scalar_tensor_tensor(out=z[:], in0=z[:], scalar=1.0, in1=q[:], op0=ALU.subtract, op1=ALU.subtract)
+                zs.append(z)
+                ks.append(k)
+            cc = half.tile([P, 4, N], BF16, name="cc")
+            for r in range(4):
+                nc.vector.scalar_tensor_tensor(
+                    out=cc[:, r, :], in0=zs[r % 2][:], scalar=0.0, in1=ks[1 - r % 2][:],
+                    op0=(ALU.max if r < 2 else ALU.min), op1=(ALU.add if r < 2 else ALU.subtract),
+                )
+            flat = cc[:].rearrange("p r n -> p (r n)")
+            nc.vector.tensor_tensor(out=flat, in0=flat, in1=mask[:].rearrange("p r n -> p (r n)"), op=ALU.mult)
+            planes = half.tile([P, L, N], BF16, align_bytes=64, name="planes")
+            b_codes = code.tile([P, L, N // 4], U32, align_bytes=64, name="b_codes")
+            b_scales = code.tile([P, L, N // 4], U8, align_bytes=64, name="b_scales")
+            for h in range(2):
+                sl = slice(4 * h, 4 * h + 4)
+                nc.vector.tensor_scalar(
+                    out=planes[:, sl, :].rearrange("p r n -> p (r n)"), in0=flat,
+                    scalar1=(2.0 if h == 0 else -2.0), scalar2=0.0, op0=ALU.mult, op1=ALU.max,
+                )
+            for h in range(2):
+                sl = slice(4 * h, 4 * h + 4)
+                quantise(
+                    planes[:, sl, :].rearrange("p r n -> p (r n)"),
+                    b_codes[:, sl, :].rearrange("p r n -> p (r n)"),
+                    b_scales[:, sl, :].rearrange("p r n -> p (r n)"),
+                )
+            return b_codes, b_scales
+
+        def multiply(c, b_codes, b_scales):
+            for n in range(NB):
+                cols = slice(n * P, (n + 1) * P)
+                acc = pa.tile([P, O], F32, name="acc")
+                nc.tensor.matmul_mx(
+                    out=acc[:], lhsT=x_codes[:, c, cols].bitcast(FP8X4), lhsT_scale=x_scales[:, c, cols],
+                    rhs=bw_codes[:].bitcast(FP8X4), rhs_scale=bw_scales[:], start=True, stop=False,
+                )
+                for l in range(L):
+                    nc.tensor.matmul_mx(
+                        out=acc[:], lhsT=b_codes[:, l, cols].bitcast(FP8X4), lhsT_scale=b_scales[:, l, cols],
+                        rhs=w_codes[:, l, :].bitcast(FP8X4), rhs_scale=w_scales[:, l, :],
+                        start=False, stop=(l == L - 1),
+                    )
+                r = res.tile([P, O], F32, name="r")
+                nc.scalar.copy(out=r[:], in_=acc[:])
+                row = (c * NB + n) * P
+                nc.sync.dma_start(out=out[row : row + P, :], in_=r[:])
+
+        done = basis(0)
+        weights(0)
+        weights(1)
+        base_weights()
+        done1 = basis(1)
+        weights(2)
+        weights(3)
+        multiply(0, done[0], done[1])
+        multiply(1, done1[0], done1[1])
+        for c in range(2, CH):
+            d = basis(c)
+            multiply(c, d[0], d[1])

@@ -1,4 +1,5 @@
 import math
+from contextlib import ExitStack
 
 import concourse.mybir as mybir
 from concourse.masks import make_identity
@@ -15,161 +16,304 @@ P = 128
 B, I, O, L = 1024, 512, 512, 8
 FLOPS = 2 * B * O * (I + I * L)
 
-CH = 4
-NB = B // P // CH
-N = NB * P * 4
+MANUAL = True
+CHUNKS = (1, 2, 2, 2, 1)
+SIGN_ON_SCALAR = (3, 4)
+W4 = P * 4
 S3 = 1.0 / math.sqrt(3.0)
 KNOT = (-0.6, -0.2, 0.2, 0.6)
+RS = (0, 2, 1, 3)
+PLANE = (0, 2, 4, 6, 1, 3, 5, 7)
 
 
 def tile_kanlayer_kernel(tc, x, base_weight, spline_weight, out):
     nc = tc.nc
-    with tc.tile_pool(name="keep", bufs=1) as keep, tc.tile_pool(name="wave", bufs=2) as wave, tc.tile_pool(
-        name="half", bufs=1
-    ) as half, tc.tile_pool(name="grp", bufs=2) as grp, tc.tile_pool(name="code", bufs=2) as code, tc.tile_pool(
-        name="res", bufs=3
-    ) as res, tc.psum_pool(name="pt", bufs=2) as pt, tc.psum_pool(name="pw", bufs=3) as pw, tc.psum_pool(
-        name="pa", bufs=3
-    ) as pa:
+    nch = len(CHUNKS)
+    first = [sum(CHUNKS[:c]) for c in range(nch)]
+    with ExitStack() as ctx:
+        keep = ctx.enter_context(tc.tile_pool(name="keep", bufs=1))
+        wave = ctx.enter_context(tc.tile_pool(name="wave", bufs=2))
+        half = ctx.enter_context(tc.tile_pool(name="half", bufs=1))
+        grp = ctx.enter_context(tc.tile_pool(name="grp", bufs=2))
+        res = ctx.enter_context(tc.tile_pool(name="res", bufs=5))
+        stage = ctx.enter_context(tc.psum_pool(name="stage", bufs=3))
+        pa = ctx.enter_context(tc.psum_pool(name="pa", bufs=5))
+        if MANUAL:
+            ctx.enter_context(tc.manual_schedule())
+
         ident = keep.tile([P, P], F32)
         make_identity(nc, ident[:])
 
-        x_raw = keep.tile([P, CH * NB, I], BF16)
+        x_raw = keep.tile([P, B // P, I], BF16)
         x_rows = x.rearrange("(n p) i -> p n i", p=P)
         bw_raw = keep.tile([P, O // P, I], BF16)
         sw_raw = [keep.tile([P, I * L], BF16, name="sw_raw%d" % m) for m in range(O // P)]
         sw_rows = spline_weight.rearrange("(m p) i l -> m p (i l)", p=P)
-        nc.sync.dma_start(out=x_raw[:, 0:4, :], in_=x_rows[:, 0:4, :])
-        nc.sync.dma_start(out=sw_raw[0][:], in_=sw_rows[0])
-        nc.sync.dma_start(out=x_raw[:, 4:8, :], in_=x_rows[:, 4:8, :])
-        nc.sync.dma_start(out=sw_raw[1][:], in_=sw_rows[1])
+        nc.sync.dma_start(out=x_raw[:, 0:2, :], in_=x_rows[:, 0:2, :])
+        nc.sync.dma_start(out=x_raw[:, 2:8, :], in_=x_rows[:, 2:8, :])
         nc.sync.dma_start(out=bw_raw[:], in_=base_weight.rearrange("(m p) i -> p m i", p=P))
-        nc.sync.dma_start(out=sw_raw[2][:], in_=sw_rows[2])
-        nc.sync.dma_start(out=sw_raw[3][:], in_=sw_rows[3])
+        for m in range(O // P):
+            nc.sync.dma_start(out=sw_raw[m][:], in_=sw_rows[m])
 
-        xg = keep.tile([P, CH, N], BF16, align_bytes=64)
-        x_codes = keep.tile([P, CH, N // 4], U32, align_bytes=64)
-        x_scales = keep.tile([P, CH, N // 4], U8, align_bytes=64)
-        bwg = keep.tile([P, 2, N], BF16, align_bytes=64)
+        xg = keep.tile([P, B // P, W4], BF16, align_bytes=64)
+        x_codes = keep.tile([P, B // P, P], U32, align_bytes=64)
+        x_scales = keep.tile([P, B // P, P], U8, align_bytes=64)
+        bwg = keep.tile([P, O // P, W4], BF16, align_bytes=64)
         bw_codes = keep.tile([P, O], U32, align_bytes=64)
         bw_scales = keep.tile([P, O], U8, align_bytes=64)
         w_codes = keep.tile([P, L, O], U32, align_bytes=64)
         w_scales = keep.tile([P, L, O], U8, align_bytes=64)
-
-        def turn_rows(raw_words, dst):
-            bank = pt.tile([P, NB, 2, P], F32, name="bank")
-            for n in range(NB):
-                for u in range(2):
-                    nc.tensor.transpose(bank[:, n, u, :], raw_words[:, n, u * P : (u + 1) * P], ident[:])
-            nc.scalar.copy(
-                out=dst.bitcast(F32).rearrange("p (n b u) -> p n b u", n=NB, u=2),
-                in_=bank[:].rearrange("p n u b -> p n b u"),
-            )
+        b_codes = [keep.tile([P, L, CHUNKS[c] * P], U32, align_bytes=64, name="b_codes%d" % c) for c in range(nch)]
+        b_scales = [keep.tile([P, L, CHUNKS[c] * P], U8, align_bytes=64, name="b_scales%d" % c) for c in range(nch)]
 
         xw = x_raw[:].bitcast(F32)
-        for c in range(CH):
-            turn_rows(xw[:, c * NB : (c + 1) * NB, :], xg[:, c, :])
+        bww = bw_raw[:].bitcast(F32)
+        banks = {}
 
         def quantise(src, codes, scales):
             nc.vector.quantize_mx(out=codes.bitcast(FP8X4), scales=scales, in_=src)
 
-        def weights(m):
-            words = sw_raw[m][:].bitcast(F32).rearrange("p (u q e j) -> p u e j q", u=2, q=P, e=2, j=4)
-            g = grp.tile([P, L, P * 4], BF16, align_bytes=64, name="g")
-            for j in range(4):
-                bank = pw.tile([P, 4, P], F32, name="wbank")
+        def flat(ap):
+            return ap.rearrange("p a b -> p (a b)")
+
+        def turn_pe(key, words, pair):
+            bank = stage.tile([P, 2, 2, P], F32, name="bank", tag="stage")
+            for n in range(2):
                 for u in range(2):
-                    for e in range(2):
-                        nc.tensor.transpose(bank[:, 2 * u + e, :], words[:, u, e, j, :], ident[:])
-                nc.scalar.copy(
-                    out=g[:, 2 * j : 2 * j + 2, :].rearrange("p s (o t) -> p s o t", t=4),
-                    in_=bank[:].bitcast(BF16).rearrange("p t (o s) -> p s o t", s=2),
-                )
-            for l in range(L):
-                quantise(g[:, l, :], w_codes[:, l, m * P : (m + 1) * P], w_scales[:, l, m * P : (m + 1) * P])
+                    nc.tensor.transpose(bank[:, n, u, :], words[:, 2 * pair + n, u * P : (u + 1) * P], ident[:])
+            banks[key] = bank
 
-        def base_weights():
-            bww = bw_raw[:].bitcast(F32)
-            for h in range(2):
-                turn_rows(bww[:, h * NB : (h + 1) * NB, :], bwg[:, h, :])
-            quantise(bwg[:].rearrange("p h n -> p (h n)"), bw_codes[:], bw_scales[:])
+        def turn_act(key, dst, pair):
+            nc.scalar.copy(
+                out=flat(dst[:, 2 * pair : 2 * pair + 2, :]).bitcast(F32).rearrange("p (n b u) -> p n b u", n=2, u=2),
+                in_=banks[key][:].rearrange("p n u b -> p n b u"),
+            )
 
-        def basis(c):
-            xc = xg[:, c, :]
-            quantise(xc, x_codes[:, c, :], x_scales[:, c, :])
-            mask = half.tile([P, 4, N], BF16, name="mask")
-            for r in range(4):
-                nc.vector.tensor_scalar(
-                    out=mask[:, r, :], in0=xc, scalar1=KNOT[r], scalar2=0.5,
-                    op0=(ALU.is_lt if r < 2 else ALU.is_ge), op1=ALU.subtract,
-                )
-            zs, ks = [], []
+        def xp(pair):
+            turn_pe(("x", pair), xw, pair)
+            turn_act(("x", pair), xg, pair)
+
+        groups = {}
+
+        def w_pe(k):
+            j, m = k // 4, k % 4
+            words = sw_raw[m][:].bitcast(F32).rearrange("p (u q e j) -> p u e j q", u=2, q=P, e=2, j=4)
+            bank = stage.tile([P, 4, P], F32, name="wbank", tag="stage")
+            for u in range(2):
+                for e in range(2):
+                    nc.tensor.transpose(bank[:, 2 * u + e, :], words[:, u, e, j, :], ident[:])
+            banks[("w", k)] = bank
+
+        def w_act(k):
+            j, m = k // 4, k % 4
+            if m == 0:
+                groups[j] = grp.tile([P, 2, O, 4], BF16, align_bytes=64, name="g")
+            nc.scalar.copy(
+                out=groups[j][:, :, m * P : (m + 1) * P, :],
+                in_=banks[("w", k)][:].bitcast(BF16).rearrange("p t (o s) -> p s o t", s=2),
+            )
+
+        def w_q(j):
+            quantise(
+                groups[j][:].rearrange("p s o t -> p (s o t)"),
+                flat(w_codes[:, 2 * j : 2 * j + 2, :]),
+                flat(w_scales[:, 2 * j : 2 * j + 2, :]),
+            )
+
+        zs, qs, ks, gates, ccs = {}, {}, {}, {}, {}
+
+        def xc(c):
+            return flat(xg[:, first[c] : first[c] + CHUNKS[c], :])
+
+        def a_wave(c):
+            n = CHUNKS[c] * W4
             for w in range(2):
-                z = wave.tile([P, N], F32, name="z%d" % w)
-                q = wave.tile([P, N], F32, name="q%d" % w)
-                k = wave.tile([P, N], F32, name="k%d" % w)
-                nc.scalar.activation(out=z[:], in_=xc, func=ACT.Abs, bias=-0.5 - w, scale=2.5)
+                z = wave.tile([P, n], F32, name="z%d" % w)
+                q = wave.tile([P, n], F32, name="q%d" % w)
+                nc.scalar.activation(out=z[:], in_=xc(c), func=ACT.Abs, bias=-0.5 - w, scale=2.5)
                 nc.scalar.activation(out=z[:], in_=z[:], func=ACT.Abs, bias=-2.0, scale=1.0)
                 nc.scalar.activation(out=q[:], in_=z[:], func=ACT.Square, bias=-S3, scale=S3)
-                nc.vector.scalar_tensor_tensor(out=q[:], in0=z[:], scalar=1.0, in1=q[:], op0=ALU.subtract, op1=ALU.mult)
-                nc.scalar.activation(out=k[:], in_=q[:], func=ACT.Abs, scale=0.5)
-                nc.vector.scalar_tensor_tensor(out=z[:], in0=z[:], scalar=1.0, in1=q[:], op0=ALU.subtract, op1=ALU.subtract)
-                zs.append(z)
-                ks.append(k)
-            cc = half.tile([P, 4, N], BF16, name="cc")
-            for r in range(4):
+                zs[(c, w)] = z
+                qs[(c, w)] = q
+
+        def d_xq(c):
+            sl = slice(first[c], first[c] + CHUNKS[c])
+            quantise(xc(c), flat(x_codes[:, sl, :]), flat(x_scales[:, sl, :]))
+
+        def gate(c):
+            n = CHUNKS[c] * W4
+            g = half.tile([P, 4, n], BF16, name="gate")
+            for i, r in enumerate(RS):
+                if c in SIGN_ON_SCALAR:
+                    s = -1.0 if r < 2 else 1.0
+                    nc.scalar.activation(out=g[:, i, :], in_=xc(c), func=ACT.Sign, bias=-s * KNOT[r], scale=s)
+                else:
+                    nc.vector.tensor_scalar(
+                        out=g[:, i, :], in0=xc(c), scalar1=KNOT[r], scalar2=0.5,
+                        op0=(ALU.is_lt if r < 2 else ALU.is_ge), op1=ALU.subtract,
+                    )
+            gates[c] = g
+
+        def d_cube(c, w):
+            z, q = zs[(c, w)], qs[(c, w)]
+            nc.vector.scalar_tensor_tensor(out=q[:], in0=z[:], scalar=1.0, in1=q[:], op0=ALU.subtract, op1=ALU.mult)
+
+        def d_psi(c, w):
+            z, q = zs[(c, w)], qs[(c, w)]
+            nc.vector.scalar_tensor_tensor(out=z[:], in0=z[:], scalar=1.0, in1=q[:], op0=ALU.subtract, op1=ALU.subtract)
+
+        def d_k(c):
+            d_cube(c, 0)
+            d_cube(c, 1)
+            d_psi(c, 0)
+            d_psi(c, 1)
+
+        def a_k(c):
+            n = CHUNKS[c] * W4
+            for w in range(2):
+                k = half.tile([P, n], F32, name="k%d" % w)
+                nc.scalar.activation(out=k[:], in_=qs[(c, w)][:], func=ACT.Abs, scale=0.5)
+                ks[(c, w)] = k
+
+        def d_c1(c):
+            n = CHUNKS[c] * W4
+            cc = half.tile([P, 4, n], BF16, name="cc")
+            for i, r in enumerate(RS):
                 nc.vector.scalar_tensor_tensor(
-                    out=cc[:, r, :], in0=zs[r % 2][:], scalar=0.0, in1=ks[1 - r % 2][:],
+                    out=cc[:, i, :], in0=zs[(c, r % 2)][:], scalar=0.0, in1=ks[(c, 1 - r % 2)][:],
                     op0=(ALU.max if r < 2 else ALU.min), op1=(ALU.add if r < 2 else ALU.subtract),
                 )
-            flat = cc[:].rearrange("p r n -> p (r n)")
-            nc.vector.tensor_tensor(out=flat, in0=flat, in1=mask[:].rearrange("p r n -> p (r n)"), op=ALU.mult)
-            planes = half.tile([P, L, N], BF16, align_bytes=64, name="planes")
-            b_codes = code.tile([P, L, N // 4], U32, align_bytes=64, name="b_codes")
-            b_scales = code.tile([P, L, N // 4], U8, align_bytes=64, name="b_scales")
-            for h in range(2):
-                sl = slice(4 * h, 4 * h + 4)
-                nc.vector.tensor_scalar(
-                    out=planes[:, sl, :].rearrange("p r n -> p (r n)"), in0=flat,
-                    scalar1=(2.0 if h == 0 else -2.0), scalar2=0.0, op0=ALU.mult, op1=ALU.max,
-                )
-            for h in range(2):
-                sl = slice(4 * h, 4 * h + 4)
-                quantise(
-                    planes[:, sl, :].rearrange("p r n -> p (r n)"),
-                    b_codes[:, sl, :].rearrange("p r n -> p (r n)"),
-                    b_scales[:, sl, :].rearrange("p r n -> p (r n)"),
-                )
-            return b_codes, b_scales
+            ccs[c] = cc
 
-        def multiply(c, b_codes, b_scales):
-            for n in range(NB):
-                cols = slice(n * P, (n + 1) * P)
-                acc = pa.tile([P, O], F32, name="acc")
-                nc.tensor.matmul_mx(
-                    out=acc[:], lhsT=x_codes[:, c, cols].bitcast(FP8X4), lhsT_scale=x_scales[:, c, cols],
-                    rhs=bw_codes[:].bitcast(FP8X4), rhs_scale=bw_scales[:], start=True, stop=False,
-                )
-                for l in range(L):
-                    nc.tensor.matmul_mx(
-                        out=acc[:], lhsT=b_codes[:, l, cols].bitcast(FP8X4), lhsT_scale=b_scales[:, l, cols],
-                        rhs=w_codes[:, l, :].bitcast(FP8X4), rhs_scale=w_scales[:, l, :],
-                        start=False, stop=(l == L - 1),
+        def d_c2(c, after_first=None):
+            n = CHUNKS[c] * W4
+            cc, g = ccs[c], gates[c]
+            s = 1.0 if c in SIGN_ON_SCALAR else 2.0
+            for h in range(2):
+                f = flat(cc[:, 2 * h : 2 * h + 2, :])
+                nc.vector.tensor_tensor(out=f, in0=f, in1=flat(g[:, 2 * h : 2 * h + 2, :]), op=ALU.mult)
+            planes = half.tile([P, L, n], BF16, align_bytes=64, name="planes")
+            for h in range(2):
+                f = flat(cc[:, 2 * h : 2 * h + 2, :])
+                for v in range(2):
+                    nc.vector.tensor_scalar(
+                        out=flat(planes[:, 4 * h + 2 * v : 4 * h + 2 * v + 2, :]), in0=f,
+                        scalar1=(s if v == 0 else -s), scalar2=0.0, op0=ALU.mult, op1=ALU.max,
                     )
-                r = res.tile([P, O], F32, name="r")
-                nc.scalar.copy(out=r[:], in_=acc[:])
-                row = (c * NB + n) * P
-                nc.sync.dma_start(out=out[row : row + P, :], in_=r[:])
+            for h in range(2):
+                sl = slice(4 * h, 4 * h + 4)
+                quantise(flat(planes[:, sl, :]), flat(b_codes[c][:, sl, :]), flat(b_scales[c][:, sl, :]))
+                if h == 0 and after_first is not None:
+                    after_first()
 
-        done = basis(0)
-        weights(0)
-        weights(1)
-        base_weights()
-        done1 = basis(1)
-        weights(2)
-        weights(3)
-        multiply(0, done[0], done[1])
-        multiply(1, done1[0], done1[1])
-        for c in range(2, CH):
-            d = basis(c)
-            multiply(c, d[0], d[1])
+        accs = {}
+        count = {}
+
+        def passes(c, which):
+            for n in range(CHUNKS[c]):
+                t = first[c] + n
+                cols = slice(n * P, (n + 1) * P)
+                for l in which:
+                    if t not in accs:
+                        accs[t] = pa.tile([P, O], F32, name="acc")
+                        count[t] = 0
+                    count[t] += 1
+                    if l < 0:
+                        nc.tensor.matmul_mx(
+                            out=accs[t][:], lhsT=x_codes[:, t, :].bitcast(FP8X4), lhsT_scale=x_scales[:, t, :],
+                            rhs=bw_codes[:].bitcast(FP8X4), rhs_scale=bw_scales[:],
+                            start=(count[t] == 1), stop=(count[t] == L + 1),
+                        )
+                    else:
+                        i = PLANE.index(l)
+                        nc.tensor.matmul_mx(
+                            out=accs[t][:], lhsT=b_codes[c][:, i, cols].bitcast(FP8X4), lhsT_scale=b_scales[c][:, i, cols],
+                            rhs=w_codes[:, l, :].bitcast(FP8X4), rhs_scale=w_scales[:, l, :],
+                            start=(count[t] == 1), stop=(count[t] == L + 1),
+                        )
+
+        def finish(t):
+            r = res.tile([P, O], F32, name="r")
+            nc.scalar.copy(out=r[:], in_=accs[t][:])
+            nc.sync.dma_start(out=out[t * P : (t + 1) * P, :], in_=r[:])
+
+        xp(0)
+        a_wave(0)
+        d_xq(0)
+        gate(0)
+        xp(1)
+        d_cube(0, 0)
+        d_psi(0, 0)
+        d_cube(0, 1)
+        d_psi(0, 1)
+
+        a_k(0)
+        a_wave(1)
+        xp(2)
+        xp(3)
+        for h in range(2):
+            turn_pe(("b", h), bww, h)
+            turn_act(("b", h), bwg, h)
+        d_c1(0)
+        d_c2(0)
+        d_xq(1)
+        gate(1)
+        d_k(1)
+        for k in range(0, 3):
+            w_pe(k)
+
+        a_k(1)
+        a_wave(2)
+        for k in range(0, 8):
+            w_act(k)
+            w_pe(k + 3)
+        d_c1(1)
+        d_c2(1)
+        quantise(flat(bwg[:]), bw_codes[:], bw_scales[:])
+        w_q(0)
+        passes(0, (-1, 0, 1))
+        passes(1, (-1, 0, 1))
+        d_xq(2)
+        gate(2)
+        d_k(2)
+        w_q(1)
+        passes(0, (2, 3))
+        passes(1, (2, 3))
+
+        a_k(2)
+        a_wave(3)
+        for k in range(8, 16):
+            w_act(k)
+            if k + 3 < 16:
+                w_pe(k + 3)
+        d_c1(2)
+        d_c2(2)
+        w_q(2)
+        passes(2, (-1, 0, 1, 2, 3, 4, 5))
+        passes(0, (4, 5))
+        passes(1, (4, 5))
+        d_xq(3)
+        d_k(3)
+        w_q(3)
+        for c in range(3):
+            passes(c, (6, 7))
+
+        a_k(3)
+        gate(3)
+        a_wave(4)
+        for t in range(5):
+            finish(t)
+        d_c1(3)
+        d_c2(3)
+        gate(4)
+        passes(3, (-1, 0, 1, 2, 3, 4, 5, 6, 7))
+        d_xq(4)
+        d_k(4)
+
+        a_k(4)
+        finish(5)
+        finish(6)
+        d_c1(4)
+        d_c2(4, after_first=lambda: passes(4, (-1, 0, 2, 4, 6)))
+        passes(4, (1, 3, 5, 7))
+        finish(7)

@@ -16,14 +16,14 @@ P = 128
 B, I, O, L = 1024, 512, 512, 8
 FLOPS = 2 * B * O * (I + I * L)
 
-MANUAL = True
+MANUAL = False
 CHUNKS = (1, 2, 2, 2, 1)
 SIGN_ON_SCALAR = (3, 4)
 W4 = P * 4
 S3 = 1.0 / math.sqrt(3.0)
 KNOT = (-0.6, -0.2, 0.2, 0.6)
-RS = (0, 2, 1, 3)
-PLANE = (0, 2, 4, 6, 1, 3, 5, 7)
+RS = (1, 3, 0, 2)
+PLANE = (1, 3, 5, 7, 0, 2, 4, 6)
 
 
 def tile_kanlayer_kernel(tc, x, base_weight, spline_weight, out):
@@ -34,7 +34,7 @@ def tile_kanlayer_kernel(tc, x, base_weight, spline_weight, out):
         keep = ctx.enter_context(tc.tile_pool(name="keep", bufs=1))
         wave = ctx.enter_context(tc.tile_pool(name="wave", bufs=2))
         half = ctx.enter_context(tc.tile_pool(name="half", bufs=1))
-        grp = ctx.enter_context(tc.tile_pool(name="grp", bufs=2))
+        grp = ctx.enter_context(tc.tile_pool(name="grp", bufs=3))
         res = ctx.enter_context(tc.tile_pool(name="res", bufs=5))
         stage = ctx.enter_context(tc.psum_pool(name="stage", bufs=3))
         pa = ctx.enter_context(tc.psum_pool(name="pa", bufs=5))
@@ -89,9 +89,11 @@ def tile_kanlayer_kernel(tc, x, base_weight, spline_weight, out):
                 in_=banks[key][:].rearrange("p n u b -> p n b u"),
             )
 
-        def xp(pair):
-            turn_pe(("x", pair), xw, pair)
-            turn_act(("x", pair), xg, pair)
+        def turn_dve(key, dst, pair):
+            nc.vector.tensor_copy(
+                out=flat(dst[:, 2 * pair : 2 * pair + 2, :]).bitcast(F32).rearrange("p (n b u) -> p n b u", n=2, u=2),
+                in_=banks[key][:].rearrange("p n u b -> p n b u"),
+            )
 
         groups = {}
 
@@ -165,8 +167,8 @@ def tile_kanlayer_kernel(tc, x, base_weight, spline_weight, out):
         def d_k(c):
             d_cube(c, 0)
             d_cube(c, 1)
-            d_psi(c, 0)
             d_psi(c, 1)
+            d_psi(c, 0)
 
         def a_k(c):
             n = CHUNKS[c] * W4
@@ -185,7 +187,7 @@ def tile_kanlayer_kernel(tc, x, base_weight, spline_weight, out):
                 )
             ccs[c] = cc
 
-        def d_c2(c, after_first=None):
+        def d_c2(c, last=False):
             n = CHUNKS[c] * W4
             cc, g = ccs[c], gates[c]
             s = 1.0 if c in SIGN_ON_SCALAR else 2.0
@@ -193,18 +195,28 @@ def tile_kanlayer_kernel(tc, x, base_weight, spline_weight, out):
                 f = flat(cc[:, 2 * h : 2 * h + 2, :])
                 nc.vector.tensor_tensor(out=f, in0=f, in1=flat(g[:, 2 * h : 2 * h + 2, :]), op=ALU.mult)
             planes = half.tile([P, L, n], BF16, align_bytes=64, name="planes")
-            for h in range(2):
-                f = flat(cc[:, 2 * h : 2 * h + 2, :])
-                for v in range(2):
-                    nc.vector.tensor_scalar(
-                        out=flat(planes[:, 4 * h + 2 * v : 4 * h + 2 * v + 2, :]), in0=f,
-                        scalar1=(s if v == 0 else -s), scalar2=0.0, op0=ALU.mult, op1=ALU.max,
-                    )
-            for h in range(2):
+
+            def split(h, v):
+                nc.vector.tensor_scalar(
+                    out=flat(planes[:, 4 * h + 2 * v : 4 * h + 2 * v + 2, :]), in0=flat(cc[:, 2 * h : 2 * h + 2, :]),
+                    scalar1=(s if v == 0 else -s), scalar2=0.0, op0=ALU.mult, op1=ALU.max,
+                )
+
+            def pack(h):
                 sl = slice(4 * h, 4 * h + 4)
                 quantise(flat(planes[:, sl, :]), flat(b_codes[c][:, sl, :]), flat(b_scales[c][:, sl, :]))
-                if h == 0 and after_first is not None:
-                    after_first()
+
+            split(0, 0)
+            split(0, 1)
+            split(1, 0)
+            if last:
+                pack(0)
+                passes(c, PLANE[0:4])
+                split(1, 1)
+            else:
+                split(1, 1)
+                pack(0)
+            pack(1)
 
         accs = {}
         count = {}
@@ -237,34 +249,41 @@ def tile_kanlayer_kernel(tc, x, base_weight, spline_weight, out):
             nc.scalar.copy(out=r[:], in_=accs[t][:])
             nc.sync.dma_start(out=out[t * P : (t + 1) * P, :], in_=r[:])
 
-        xp(0)
+        turn_pe(("x", 0), xw, 0)
+        turn_act(("x", 0), xg, 0)
         a_wave(0)
         d_xq(0)
         gate(0)
-        xp(1)
+        turn_pe(("x", 1), xw, 1)
+        turn_dve(("x", 1), xg, 1)
         d_cube(0, 0)
+        turn_pe(("x", 2), xw, 2)
+        turn_dve(("x", 2), xg, 2)
         d_psi(0, 0)
         d_cube(0, 1)
         d_psi(0, 1)
+        turn_pe(("x", 3), xw, 3)
+        turn_dve(("x", 3), xg, 3)
 
         a_k(0)
         a_wave(1)
-        xp(2)
-        xp(3)
         for h in range(2):
             turn_pe(("b", h), bww, h)
             turn_act(("b", h), bwg, h)
+        for k in range(0, 3):
+            w_pe(k)
+        for k in range(0, 1):
+            w_act(k)
+            w_pe(k + 3)
         d_c1(0)
         d_c2(0)
         d_xq(1)
         gate(1)
         d_k(1)
-        for k in range(0, 3):
-            w_pe(k)
 
         a_k(1)
         a_wave(2)
-        for k in range(0, 8):
+        for k in range(1, 10):
             w_act(k)
             w_pe(k + 3)
         d_c1(1)
@@ -273,16 +292,16 @@ def tile_kanlayer_kernel(tc, x, base_weight, spline_weight, out):
         w_q(0)
         passes(0, (-1, 0, 1))
         passes(1, (-1, 0, 1))
-        d_xq(2)
-        gate(2)
-        d_k(2)
         w_q(1)
         passes(0, (2, 3))
         passes(1, (2, 3))
+        d_xq(2)
+        gate(2)
+        d_k(2)
 
         a_k(2)
         a_wave(3)
-        for k in range(8, 16):
+        for k in range(10, 16):
             w_act(k)
             if k + 3 < 16:
                 w_pe(k + 3)
@@ -308,12 +327,13 @@ def tile_kanlayer_kernel(tc, x, base_weight, spline_weight, out):
         gate(4)
         passes(3, (-1, 0, 1, 2, 3, 4, 5, 6, 7))
         d_xq(4)
+        passes(4, (-1,))
         d_k(4)
 
         a_k(4)
         finish(5)
         finish(6)
         d_c1(4)
-        d_c2(4, after_first=lambda: passes(4, (-1, 0, 2, 4, 6)))
-        passes(4, (1, 3, 5, 7))
+        d_c2(4, last=True)
+        passes(4, PLANE[4:8])
         finish(7)

@@ -16,13 +16,13 @@ P = 128
 B, I, O, L = 1024, 512, 512, 8
 FLOPS = 2 * B * O * (I + I * L)
 
-MANUAL = False
 CHUNKS = (1, 2, 2, 2, 1)
-SIGN_ON_SCALAR = (3, 4)
+SIGN_ON_SCALAR = (4,)
 W4 = P * 4
 S3 = 1.0 / math.sqrt(3.0)
 KNOT = (-0.6, -0.2, 0.2, 0.6)
 RS = (1, 3, 0, 2)
+PSI_ON_PE = ((1, 1), (1, 0), (2, 1), (2, 0), (3, 1))
 PLANE = (1, 3, 5, 7, 0, 2, 4, 6)
 
 
@@ -34,15 +34,17 @@ def tile_kanlayer_kernel(tc, x, base_weight, spline_weight, out):
         keep = ctx.enter_context(tc.tile_pool(name="keep", bufs=1))
         wave = ctx.enter_context(tc.tile_pool(name="wave", bufs=2))
         half = ctx.enter_context(tc.tile_pool(name="half", bufs=1))
-        grp = ctx.enter_context(tc.tile_pool(name="grp", bufs=3))
+        grp = ctx.enter_context(tc.tile_pool(name="grp", bufs=2))
         res = ctx.enter_context(tc.tile_pool(name="res", bufs=5))
-        stage = ctx.enter_context(tc.psum_pool(name="stage", bufs=3))
-        pa = ctx.enter_context(tc.psum_pool(name="pa", bufs=5))
-        if MANUAL:
-            ctx.enter_context(tc.manual_schedule())
+        psum = ctx.enter_context(tc.psum_pool(name="psum", bufs=8))
+        ctx.enter_context(tc.manual_schedule())
 
         ident = keep.tile([P, P], F32)
         make_identity(nc, ident[:])
+        nident = keep.tile([P, P], F32)
+        nc.gpsimd.tensor_scalar(out=nident[:], in0=ident[:], scalar1=-1.0, scalar2=0.0, op0=ALU.mult, op1=ALU.add)
+        minus = keep.tile([P, P], F32)
+        nc.gpsimd.memset(minus[:], -1.0)
 
         x_raw = keep.tile([P, B // P, I], BF16)
         x_rows = x.rearrange("(n p) i -> p n i", p=P)
@@ -77,7 +79,7 @@ def tile_kanlayer_kernel(tc, x, base_weight, spline_weight, out):
             return ap.rearrange("p a b -> p (a b)")
 
         def turn_pe(key, words, pair):
-            bank = stage.tile([P, 2, 2, P], F32, name="bank", tag="stage")
+            bank = psum.tile([P, 2, 2, P], F32, name="bank", tag="bank")
             for n in range(2):
                 for u in range(2):
                     nc.tensor.transpose(bank[:, n, u, :], words[:, 2 * pair + n, u * P : (u + 1) * P], ident[:])
@@ -100,7 +102,7 @@ def tile_kanlayer_kernel(tc, x, base_weight, spline_weight, out):
         def w_pe(k):
             j, m = k // 4, k % 4
             words = sw_raw[m][:].bitcast(F32).rearrange("p (u q e j) -> p u e j q", u=2, q=P, e=2, j=4)
-            bank = stage.tile([P, 4, P], F32, name="wbank", tag="stage")
+            bank = psum.tile([P, 4, P], F32, name="wbank", tag="bank")
             for u in range(2):
                 for e in range(2):
                     nc.tensor.transpose(bank[:, 2 * u + e, :], words[:, u, e, j, :], ident[:])
@@ -127,16 +129,15 @@ def tile_kanlayer_kernel(tc, x, base_weight, spline_weight, out):
         def xc(c):
             return flat(xg[:, first[c] : first[c] + CHUNKS[c], :])
 
-        def a_wave(c):
+        def a_wave(c, w):
             n = CHUNKS[c] * W4
-            for w in range(2):
-                z = wave.tile([P, n], F32, name="z%d" % w)
-                q = wave.tile([P, n], F32, name="q%d" % w)
-                nc.scalar.activation(out=z[:], in_=xc(c), func=ACT.Abs, bias=-0.5 - w, scale=2.5)
-                nc.scalar.activation(out=z[:], in_=z[:], func=ACT.Abs, bias=-2.0, scale=1.0)
-                nc.scalar.activation(out=q[:], in_=z[:], func=ACT.Square, bias=-S3, scale=S3)
-                zs[(c, w)] = z
-                qs[(c, w)] = q
+            z = wave.tile([P, n], F32, name="z%d" % w)
+            q = wave.tile([P, n], F32, name="q%d" % w)
+            nc.scalar.activation(out=z[:], in_=xc(c), func=ACT.Abs, bias=-0.5 - w, scale=2.5)
+            nc.scalar.activation(out=z[:], in_=z[:], func=ACT.Abs, bias=-2.0, scale=1.0)
+            nc.scalar.activation(out=q[:], in_=z[:], func=ACT.Square, bias=-S3, scale=S3)
+            zs[(c, w)] = z
+            qs[(c, w)] = q
 
         def d_xq(c):
             sl = slice(first[c], first[c] + CHUNKS[c])
@@ -144,7 +145,7 @@ def tile_kanlayer_kernel(tc, x, base_weight, spline_weight, out):
 
         def gate(c):
             n = CHUNKS[c] * W4
-            g = half.tile([P, 4, n], BF16, name="gate")
+            g = half.tile([P, 4, n], BF16, name="gate", bufs=2)
             for i, r in enumerate(RS):
                 if c in SIGN_ON_SCALAR:
                     s = -1.0 if r < 2 else 1.0
@@ -160,63 +161,77 @@ def tile_kanlayer_kernel(tc, x, base_weight, spline_weight, out):
             z, q = zs[(c, w)], qs[(c, w)]
             nc.vector.scalar_tensor_tensor(out=q[:], in0=z[:], scalar=1.0, in1=q[:], op0=ALU.subtract, op1=ALU.mult)
 
+        psis = {}
+
+        def make_psi(c, w):
+            if (c, w) in PSI_ON_PE:
+                for n in range(CHUNKS[c]):
+                    pe_psi(c, n, w)
+
         def d_psi(c, w):
             z, q = zs[(c, w)], qs[(c, w)]
             nc.vector.scalar_tensor_tensor(out=z[:], in0=z[:], scalar=1.0, in1=q[:], op0=ALU.subtract, op1=ALU.subtract)
 
-        def d_k(c):
-            d_cube(c, 0)
-            d_cube(c, 1)
-            d_psi(c, 1)
-            d_psi(c, 0)
-
-        def a_k(c):
-            n = CHUNKS[c] * W4
-            for w in range(2):
-                k = half.tile([P, n], F32, name="k%d" % w)
-                nc.scalar.activation(out=k[:], in_=qs[(c, w)][:], func=ACT.Abs, scale=0.5)
-                ks[(c, w)] = k
-
-        def d_c1(c):
-            n = CHUNKS[c] * W4
-            cc = half.tile([P, 4, n], BF16, name="cc")
-            for i, r in enumerate(RS):
-                nc.vector.scalar_tensor_tensor(
-                    out=cc[:, i, :], in0=zs[(c, r % 2)][:], scalar=0.0, in1=ks[(c, 1 - r % 2)][:],
-                    op0=(ALU.max if r < 2 else ALU.min), op1=(ALU.add if r < 2 else ALU.subtract),
+        def pe_psi(c, n, w):
+            sl = slice(n * W4, (n + 1) * W4)
+            bank = psum.tile([P, W4], F32, name="psi", tag="bank")
+            nc.tensor.matmul(bank[:], lhsT=ident[:], rhs=zs[(c, w)][:, sl], start=True, stop=False)
+            for h in range(4):
+                nc.tensor.matmul(
+                    bank[:, h * P : (h + 1) * P], lhsT=minus[:], rhs=ident[:], start=False, stop=False, is_transpose=True
                 )
-            ccs[c] = cc
+            nc.tensor.matmul(bank[:], lhsT=nident[:], rhs=qs[(c, w)][:, sl], start=False, stop=True)
+            psis[(c, n, w)] = bank
 
-        def d_c2(c, last=False):
-            n = CHUNKS[c] * W4
-            cc, g = ccs[c], gates[c]
+        def a_k(c, w):
+            k = half.tile([P, CHUNKS[c] * W4], F32, name="k%d" % w)
+            nc.scalar.activation(out=k[:], in_=qs[(c, w)][:], func=ACT.Abs, scale=0.5)
+            ks[(c, w)] = k
+
+        def d_c1(c, w):
+            if c not in ccs:
+                ccs[c] = half.tile([P, 4, CHUNKS[c] * W4], BF16, name="cc")
+            n = CHUNKS[c]
+            parts = [(m, slice(m * W4, (m + 1) * W4)) for m in range(n)] if (c, 0, w) in psis else [(None, slice(0, n * W4))]
+            for m, sl in parts:
+                psi = zs[(c, w)][:, sl] if m is None else psis[(c, m, w)][:]
+                for i, r in enumerate(RS):
+                    if r % 2 == w:
+                        nc.vector.scalar_tensor_tensor(
+                            out=ccs[c][:, i, sl], in0=psi, scalar=0.0, in1=ks[(c, 1 - w)][:, sl],
+                            op0=(ALU.max if r < 2 else ALU.min), op1=(ALU.add if r < 2 else ALU.subtract),
+                        )
+
+        plane = {}
+
+        def d_mult(c, h):
+            f = flat(ccs[c][:, 2 * h : 2 * h + 2, :])
+            nc.vector.tensor_tensor(out=f, in0=f, in1=flat(gates[c][:, 2 * h : 2 * h + 2, :]), op=ALU.mult)
+
+        def d_split(c, h, v):
+            if c not in plane:
+                plane[c] = half.tile([P, L, CHUNKS[c] * W4], BF16, align_bytes=64, name="planes")
             s = 1.0 if c in SIGN_ON_SCALAR else 2.0
-            for h in range(2):
-                f = flat(cc[:, 2 * h : 2 * h + 2, :])
-                nc.vector.tensor_tensor(out=f, in0=f, in1=flat(g[:, 2 * h : 2 * h + 2, :]), op=ALU.mult)
-            planes = half.tile([P, L, n], BF16, align_bytes=64, name="planes")
+            nc.vector.tensor_scalar(
+                out=flat(plane[c][:, 4 * h + 2 * v : 4 * h + 2 * v + 2, :]), in0=flat(ccs[c][:, 2 * h : 2 * h + 2, :]),
+                scalar1=(s if v == 0 else -s), scalar2=0.0, op0=ALU.mult, op1=ALU.max,
+            )
 
-            def split(h, v):
-                nc.vector.tensor_scalar(
-                    out=flat(planes[:, 4 * h + 2 * v : 4 * h + 2 * v + 2, :]), in0=flat(cc[:, 2 * h : 2 * h + 2, :]),
-                    scalar1=(s if v == 0 else -s), scalar2=0.0, op0=ALU.mult, op1=ALU.max,
-                )
+        def d_pack(c, lo, hi):
+            sl = slice(lo, hi)
+            quantise(flat(plane[c][:, sl, :]), flat(b_codes[c][:, sl, :]), flat(b_scales[c][:, sl, :]))
 
-            def pack(h):
-                sl = slice(4 * h, 4 * h + 4)
-                quantise(flat(planes[:, sl, :]), flat(b_codes[c][:, sl, :]), flat(b_scales[c][:, sl, :]))
+        def c2a(c):
+            d_mult(c, 0)
+            d_mult(c, 1)
+            d_split(c, 0, 0)
+            d_split(c, 0, 1)
 
-            split(0, 0)
-            split(0, 1)
-            split(1, 0)
-            if last:
-                pack(0)
-                passes(c, PLANE[0:4])
-                split(1, 1)
-            else:
-                split(1, 1)
-                pack(0)
-            pack(1)
+        def c2b(c):
+            d_split(c, 1, 0)
+            d_split(c, 1, 1)
+            d_pack(c, 0, 4)
+            d_pack(c, 4, 8)
 
         accs = {}
         count = {}
@@ -227,7 +242,7 @@ def tile_kanlayer_kernel(tc, x, base_weight, spline_weight, out):
                 cols = slice(n * P, (n + 1) * P)
                 for l in which:
                     if t not in accs:
-                        accs[t] = pa.tile([P, O], F32, name="acc")
+                        accs[t] = psum.tile([P, O], F32, name="acc", tag="bank")
                         count[t] = 0
                     count[t] += 1
                     if l < 0:
@@ -249,91 +264,159 @@ def tile_kanlayer_kernel(tc, x, base_weight, spline_weight, out):
             nc.scalar.copy(out=r[:], in_=accs[t][:])
             nc.sync.dma_start(out=out[t * P : (t + 1) * P, :], in_=r[:])
 
+        ahead = [0]
+
+        def w_ahead(k):
+            for j in range(ahead[0], min(k, 16)):
+                w_pe(j)
+                ahead[0] = j + 1
+
+        def w_job(k):
+            w_act(k)
+            w_ahead(k + 3)
+
         turn_pe(("x", 0), xw, 0)
         turn_act(("x", 0), xg, 0)
-        a_wave(0)
+        a_wave(0, 1)
+        a_wave(0, 0)
         d_xq(0)
         gate(0)
         turn_pe(("x", 1), xw, 1)
         turn_dve(("x", 1), xg, 1)
-        d_cube(0, 0)
         turn_pe(("x", 2), xw, 2)
         turn_dve(("x", 2), xg, 2)
-        d_psi(0, 0)
         d_cube(0, 1)
-        d_psi(0, 1)
         turn_pe(("x", 3), xw, 3)
         turn_dve(("x", 3), xg, 3)
-
-        a_k(0)
-        a_wave(1)
         for h in range(2):
             turn_pe(("b", h), bww, h)
-            turn_act(("b", h), bwg, h)
-        for k in range(0, 3):
-            w_pe(k)
-        for k in range(0, 1):
-            w_act(k)
-            w_pe(k + 3)
-        d_c1(0)
-        d_c2(0)
+        w_ahead(2)
+        d_psi(0, 1)
+        d_cube(0, 0)
+        a_k(0, 1)
         d_xq(1)
+        d_psi(0, 0)
+        a_k(0, 0)
+        a_wave(1, 1)
+        d_c1(0, 1)
+        d_c1(0, 0)
         gate(1)
-        d_k(1)
-
-        a_k(1)
-        a_wave(2)
-        for k in range(1, 10):
-            w_act(k)
-            w_pe(k + 3)
-        d_c1(1)
-        d_c2(1)
+        d_mult(0, 0)
+        a_wave(1, 0)
+        d_cube(1, 1)
+        make_psi(1, 1)
+        a_k(1, 1)
+        for h in range(2):
+            turn_act(("b", h), bwg, h)
+        d_mult(0, 1)
+        d_split(0, 0, 0)
+        d_split(0, 0, 1)
+        d_split(0, 1, 0)
+        d_split(0, 1, 1)
+        d_pack(0, 0, 4)
+        d_cube(1, 0)
+        w_ahead(3)
+        make_psi(1, 0)
+        a_k(1, 0)
+        a_wave(2, 1)
+        a_wave(2, 0)
+        gate(2)
+        d_xq(2)
+        d_c1(1, 1)
+        d_xq(3)
+        d_pack(0, 4, 8)
+        d_c1(1, 0)
+        d_cube(2, 1)
+        make_psi(2, 1)
+        a_k(2, 1)
+        c2a(1)
+        w_job(0)
+        d_cube(2, 0)
+        w_ahead(4)
+        make_psi(2, 0)
+        w_job(1)
+        a_k(2, 0)
+        c2b(1)
+        w_job(2)
+        w_job(3)
         quantise(flat(bwg[:]), bw_codes[:], bw_scales[:])
         w_q(0)
+        a_wave(3, 1)
+        a_wave(3, 0)
+        d_c1(2, 1)
+        d_c1(2, 0)
         passes(0, (-1, 0, 1))
         passes(1, (-1, 0, 1))
+        d_cube(3, 1)
+        w_ahead(7)
+        make_psi(3, 1)
+        w_job(4)
+        a_k(3, 1)
+        c2a(2)
+        w_job(5)
+        w_job(6)
+        d_cube(3, 0)
+        a_k(3, 0)
+        w_job(7)
+        c2b(2)
+        d_psi(3, 0)
+        gate(3)
+        for k in range(8, 12):
+            w_job(k)
         w_q(1)
+        for k in range(12, 14):
+            w_job(k)
         passes(0, (2, 3))
         passes(1, (2, 3))
-        d_xq(2)
-        gate(2)
-        d_k(2)
-
-        a_k(2)
-        a_wave(3)
-        for k in range(10, 16):
-            w_act(k)
-            if k + 3 < 16:
-                w_pe(k + 3)
-        d_c1(2)
-        d_c2(2)
+        d_xq(4)
         w_q(2)
-        passes(2, (-1, 0, 1, 2, 3, 4, 5))
+        for k in range(14, 16):
+            w_job(k)
+        a_wave(4, 1)
+        a_wave(4, 0)
+        d_c1(3, 0)
+        d_c1(3, 1)
         passes(0, (4, 5))
         passes(1, (4, 5))
-        d_xq(3)
-        d_k(3)
+        passes(2, (-1, 0, 1, 2, 3, 4, 5))
+        d_mult(3, 0)
         w_q(3)
+        d_split(3, 0, 0)
+        d_split(3, 0, 1)
+        d_cube(4, 1)
+        d_mult(3, 1)
+        a_k(4, 1)
         for c in range(3):
             passes(c, (6, 7))
-
-        a_k(3)
-        gate(3)
-        a_wave(4)
+        passes(3, (-1,))
+        passes(4, (-1,))
+        d_pack(3, 0, 4)
+        passes(3, PLANE[0:4])
+        d_cube(4, 0)
+        a_k(4, 0)
+        gate(4)
+        d_split(3, 1, 0)
+        d_split(3, 1, 1)
+        d_psi(4, 1)
+        d_pack(3, 4, 8)
+        d_psi(4, 0)
         for t in range(5):
             finish(t)
-        d_c1(3)
-        d_c2(3)
-        gate(4)
-        passes(3, (-1, 0, 1, 2, 3, 4, 5, 6, 7))
-        d_xq(4)
-        passes(4, (-1,))
-        d_k(4)
-
-        a_k(4)
+        passes(3, PLANE[4:8])
+        d_c1(4, 1)
+        d_c1(4, 0)
         finish(5)
         finish(6)
-        d_c1(4)
-        d_c2(4, last=True)
-        passes(4, PLANE[4:8])
+        d_mult(4, 0)
+        d_mult(4, 1)
+        d_split(4, 0, 0)
+        d_split(4, 0, 1)
+        d_split(4, 1, 0)
+        d_pack(4, 0, 4)
+        passes(4, PLANE[0:4])
+        d_split(4, 1, 1)
+        d_pack(4, 4, 6)
+        passes(4, PLANE[4:6])
+        d_pack(4, 6, 8)
+        passes(4, PLANE[6:8])
         finish(7)

@@ -22,7 +22,7 @@ W4 = P * 4
 S3 = 1.0 / math.sqrt(3.0)
 KNOT = (-0.6, -0.2, 0.2, 0.6)
 RS = (1, 3, 0, 2)
-PSI_ON_PE = ((1, 1), (1, 0), (2, 1), (2, 0), (3, 1))
+PSI_ON_PE = ((0, 1), (1, 1), (1, 0), (2, 1), (2, 0), (3, 1), (4, 1))
 PLANE = (1, 3, 5, 7, 0, 2, 4, 6)
 
 
@@ -35,7 +35,7 @@ def tile_kanlayer_kernel(tc, x, base_weight, spline_weight, out):
         wave = ctx.enter_context(tc.tile_pool(name="wave", bufs=2))
         half = ctx.enter_context(tc.tile_pool(name="half", bufs=1))
         grp = ctx.enter_context(tc.tile_pool(name="grp", bufs=2))
-        res = ctx.enter_context(tc.tile_pool(name="res", bufs=5))
+        res = ctx.enter_context(tc.tile_pool(name="res", bufs=7))
         psum = ctx.enter_context(tc.psum_pool(name="psum", bufs=8))
         ctx.enter_context(tc.manual_schedule())
 
@@ -51,8 +51,8 @@ def tile_kanlayer_kernel(tc, x, base_weight, spline_weight, out):
         bw_raw = keep.tile([P, O // P, I], BF16)
         sw_raw = [keep.tile([P, I * L], BF16, name="sw_raw%d" % m) for m in range(O // P)]
         sw_rows = spline_weight.rearrange("(m p) i l -> m p (i l)", p=P)
-        nc.sync.dma_start(out=x_raw[:, 0:2, :], in_=x_rows[:, 0:2, :])
-        nc.sync.dma_start(out=x_raw[:, 2:8, :], in_=x_rows[:, 2:8, :])
+        for lo, hi in ((0, 1), (1, 3), (3, 8)):
+            nc.sync.dma_start(out=x_raw[:, lo:hi, :], in_=x_rows[:, lo:hi, :])
         nc.sync.dma_start(out=bw_raw[:], in_=base_weight.rearrange("(m p) i -> p m i", p=P))
         for m in range(O // P):
             nc.sync.dma_start(out=sw_raw[m][:], in_=sw_rows[m])
@@ -78,23 +78,17 @@ def tile_kanlayer_kernel(tc, x, base_weight, spline_weight, out):
         def flat(ap):
             return ap.rearrange("p a b -> p (a b)")
 
-        def turn_pe(key, words, pair):
+        def turn_pe(key, words, lo, hi):
             bank = psum.tile([P, 2, 2, P], F32, name="bank", tag="bank")
-            for n in range(2):
+            for n in range(lo, hi):
                 for u in range(2):
-                    nc.tensor.transpose(bank[:, n, u, :], words[:, 2 * pair + n, u * P : (u + 1) * P], ident[:])
+                    nc.tensor.transpose(bank[:, n - lo, u, :], words[:, n, u * P : (u + 1) * P], ident[:])
             banks[key] = bank
 
-        def turn_act(key, dst, pair):
-            nc.scalar.copy(
-                out=flat(dst[:, 2 * pair : 2 * pair + 2, :]).bitcast(F32).rearrange("p (n b u) -> p n b u", n=2, u=2),
-                in_=banks[key][:].rearrange("p n u b -> p n b u"),
-            )
-
-        def turn_dve(key, dst, pair):
-            nc.vector.tensor_copy(
-                out=flat(dst[:, 2 * pair : 2 * pair + 2, :]).bitcast(F32).rearrange("p (n b u) -> p n b u", n=2, u=2),
-                in_=banks[key][:].rearrange("p n u b -> p n b u"),
+        def turn_out(copy, key, dst, lo, hi):
+            copy(
+                out=flat(dst[:, lo:hi, :]).bitcast(F32).rearrange("p (n b u) -> p n b u", n=hi - lo, u=2),
+                in_=banks[key][:, 0 : hi - lo].rearrange("p n u b -> p n b u"),
             )
 
         groups = {}
@@ -129,11 +123,18 @@ def tile_kanlayer_kernel(tc, x, base_weight, spline_weight, out):
         def xc(c):
             return flat(xg[:, first[c] : first[c] + CHUNKS[c], :])
 
-        def a_wave(c, w):
+        def a_wave(c, w, bank=None):
             n = CHUNKS[c] * W4
             z = wave.tile([P, n], F32, name="z%d" % w)
             q = wave.tile([P, n], F32, name="q%d" % w)
-            nc.scalar.activation(out=z[:], in_=xc(c), func=ACT.Abs, bias=-0.5 - w, scale=2.5)
+            if bank is None:
+                nc.scalar.activation(out=z[:], in_=xc(c), func=ACT.Abs, bias=-0.5 - w, scale=2.5)
+            else:
+                nc.scalar.activation(
+                    out=z[:].rearrange("p (b u e) -> p b u e", u=2, e=2),
+                    in_=bank[:, 0].bitcast(BF16).rearrange("p u (b e) -> p b u e", e=2),
+                    func=ACT.Abs, bias=-0.5 - w, scale=2.5,
+                )
             nc.scalar.activation(out=z[:], in_=z[:], func=ACT.Abs, bias=-2.0, scale=1.0)
             nc.scalar.activation(out=q[:], in_=z[:], func=ACT.Square, bias=-S3, scale=S3)
             zs[(c, w)] = z
@@ -236,33 +237,41 @@ def tile_kanlayer_kernel(tc, x, base_weight, spline_weight, out):
         accs = {}
         count = {}
 
-        def passes(c, which):
+        def passes(c, which, half=None):
             for n in range(CHUNKS[c]):
                 t = first[c] + n
                 cols = slice(n * P, (n + 1) * P)
+                key = t if half is None else (t, half)
+                oc = slice(0, O) if half is None else slice(half * (O // 2), (half + 1) * (O // 2))
                 for l in which:
-                    if t not in accs:
-                        accs[t] = psum.tile([P, O], F32, name="acc", tag="bank")
-                        count[t] = 0
-                    count[t] += 1
+                    if key not in accs:
+                        accs[key] = psum.tile([P, O], F32, name="acc", tag="bank")
+                        count[key] = 0
+                    count[key] += 1
+                    acc = accs[key][:, 0 : oc.stop - oc.start]
                     if l < 0:
                         nc.tensor.matmul_mx(
-                            out=accs[t][:], lhsT=x_codes[:, t, :].bitcast(FP8X4), lhsT_scale=x_scales[:, t, :],
-                            rhs=bw_codes[:].bitcast(FP8X4), rhs_scale=bw_scales[:],
-                            start=(count[t] == 1), stop=(count[t] == L + 1),
+                            out=acc, lhsT=x_codes[:, t, :].bitcast(FP8X4), lhsT_scale=x_scales[:, t, :],
+                            rhs=bw_codes[:, oc].bitcast(FP8X4), rhs_scale=bw_scales[:, oc],
+                            start=(count[key] == 1), stop=(count[key] == L + 1),
                         )
                     else:
                         i = PLANE.index(l)
                         nc.tensor.matmul_mx(
-                            out=accs[t][:], lhsT=b_codes[c][:, i, cols].bitcast(FP8X4), lhsT_scale=b_scales[c][:, i, cols],
-                            rhs=w_codes[:, l, :].bitcast(FP8X4), rhs_scale=w_scales[:, l, :],
-                            start=(count[t] == 1), stop=(count[t] == L + 1),
+                            out=acc, lhsT=b_codes[c][:, i, cols].bitcast(FP8X4), lhsT_scale=b_scales[c][:, i, cols],
+                            rhs=w_codes[:, l, oc].bitcast(FP8X4), rhs_scale=w_scales[:, l, oc],
+                            start=(count[key] == 1), stop=(count[key] == L + 1),
                         )
 
         def finish(t):
             r = res.tile([P, O], F32, name="r")
             nc.scalar.copy(out=r[:], in_=accs[t][:])
             nc.sync.dma_start(out=out[t * P : (t + 1) * P, :], in_=r[:])
+
+        def finish_half(t, half, copy):
+            r = res.tile([P, O // 2], F32, name="rh", bufs=2)
+            copy(out=r[:], in_=accs[(t, half)][:, 0 : O // 2])
+            nc.sync.dma_start(out=out[t * P : (t + 1) * P, half * (O // 2) : (half + 1) * (O // 2)], in_=r[:])
 
         ahead = [0]
 
@@ -275,45 +284,48 @@ def tile_kanlayer_kernel(tc, x, base_weight, spline_weight, out):
             w_act(k)
             w_ahead(k + 3)
 
-        turn_pe(("x", 0), xw, 0)
-        turn_act(("x", 0), xg, 0)
-        a_wave(0, 1)
+        turn_pe("xs", xw, 0, 1)
+        turn_pe("xv", xw, 0, 1)
+        turn_out(nc.vector.tensor_copy, "xv", xg, 0, 1)
+        a_wave(0, 1, banks["xs"])
         a_wave(0, 0)
         d_xq(0)
         gate(0)
-        turn_pe(("x", 1), xw, 1)
-        turn_dve(("x", 1), xg, 1)
-        turn_pe(("x", 2), xw, 2)
-        turn_dve(("x", 2), xg, 2)
+        turn_pe("x1", xw, 1, 2)
+        turn_out(nc.vector.tensor_copy, "x1", xg, 1, 2)
+        turn_pe("x2", xw, 2, 4)
+        turn_out(nc.vector.tensor_copy, "x2", xg, 2, 4)
+        turn_pe("x4", xw, 4, 6)
+        turn_pe("x6", xw, 6, 8)
         d_cube(0, 1)
-        turn_pe(("x", 3), xw, 3)
-        turn_dve(("x", 3), xg, 3)
-        for h in range(2):
-            turn_pe(("b", h), bww, h)
-        w_ahead(2)
-        d_psi(0, 1)
-        d_cube(0, 0)
+        make_psi(0, 1)
+        turn_out(nc.vector.tensor_copy, "x4", xg, 4, 6)
         a_k(0, 1)
-        d_xq(1)
+        d_cube(0, 0)
+        turn_out(nc.vector.tensor_copy, "x6", xg, 6, 8)
+        turn_pe("b0", bww, 0, 2)
+        turn_pe("b1", bww, 2, 4)
+        w_ahead(2)
         d_psi(0, 0)
         a_k(0, 0)
+        d_xq(1)
         a_wave(1, 1)
-        d_c1(0, 1)
         d_c1(0, 0)
+        d_c1(0, 1)
         gate(1)
-        d_mult(0, 0)
+        d_mult(0, 1)
         a_wave(1, 0)
         d_cube(1, 1)
         make_psi(1, 1)
         a_k(1, 1)
-        for h in range(2):
-            turn_act(("b", h), bwg, h)
-        d_mult(0, 1)
-        d_split(0, 0, 0)
-        d_split(0, 0, 1)
+        turn_out(nc.scalar.copy, "b0", bwg, 0, 2)
+        turn_out(nc.scalar.copy, "b1", bwg, 2, 4)
+        d_mult(0, 0)
         d_split(0, 1, 0)
         d_split(0, 1, 1)
-        d_pack(0, 0, 4)
+        d_split(0, 0, 0)
+        d_split(0, 0, 1)
+        d_pack(0, 4, 8)
         d_cube(1, 0)
         w_ahead(3)
         make_psi(1, 0)
@@ -324,7 +336,8 @@ def tile_kanlayer_kernel(tc, x, base_weight, spline_weight, out):
         d_xq(2)
         d_c1(1, 1)
         d_xq(3)
-        d_pack(0, 4, 8)
+        d_pack(0, 0, 4)
+        quantise(flat(bwg[:]), bw_codes[:], bw_scales[:])
         d_c1(1, 0)
         d_cube(2, 1)
         make_psi(2, 1)
@@ -339,7 +352,6 @@ def tile_kanlayer_kernel(tc, x, base_weight, spline_weight, out):
         c2b(1)
         w_job(2)
         w_job(3)
-        quantise(flat(bwg[:]), bw_codes[:], bw_scales[:])
         w_q(0)
         a_wave(3, 1)
         a_wave(3, 0)
@@ -381,42 +393,44 @@ def tile_kanlayer_kernel(tc, x, base_weight, spline_weight, out):
         passes(2, (-1, 0, 1, 2, 3, 4, 5))
         d_mult(3, 0)
         w_q(3)
+        d_cube(4, 1)
+        make_psi(4, 1)
+        a_k(4, 1)
         d_split(3, 0, 0)
         d_split(3, 0, 1)
-        d_cube(4, 1)
-        d_mult(3, 1)
-        a_k(4, 1)
-        for c in range(3):
-            passes(c, (6, 7))
-        passes(3, (-1,))
-        passes(4, (-1,))
-        d_pack(3, 0, 4)
-        passes(3, PLANE[0:4])
         d_cube(4, 0)
         a_k(4, 0)
+        make_psi(4, 0)
+        d_mult(3, 1)
         gate(4)
-        d_split(3, 1, 0)
-        d_split(3, 1, 1)
-        d_psi(4, 1)
-        d_pack(3, 4, 8)
-        d_psi(4, 0)
+        for c in range(3):
+            passes(c, (6, 7))
         for t in range(5):
             finish(t)
-        passes(3, PLANE[4:8])
+        d_pack(3, 0, 4)
+        d_split(3, 1, 0)
+        d_split(3, 1, 1)
+        d_psi(4, 0)
         d_c1(4, 1)
+        d_pack(3, 4, 8)
         d_c1(4, 0)
-        finish(5)
-        finish(6)
         d_mult(4, 0)
         d_mult(4, 1)
         d_split(4, 0, 0)
         d_split(4, 0, 1)
         d_split(4, 1, 0)
         d_pack(4, 0, 4)
-        passes(4, PLANE[0:4])
+        passes(3, (-1,) + PLANE)
+        finish(5)
+        finish(6)
+        for half in range(2):
+            passes(4, (-1,) + PLANE[0:4], half)
         d_split(4, 1, 1)
         d_pack(4, 4, 6)
-        passes(4, PLANE[4:6])
+        for half in range(2):
+            passes(4, PLANE[4:6], half)
         d_pack(4, 6, 8)
-        passes(4, PLANE[6:8])
-        finish(7)
+        for half in range(2):
+            passes(4, PLANE[6:8], half)
+        finish_half(7, 0, nc.scalar.copy)
+        finish_half(7, 1, nc.vector.tensor_copy)

@@ -17,10 +17,12 @@ B, I, O, L = 1024, 512, 512, 8
 FLOPS = 2 * B * O * (I + I * L)
 
 CHUNKS = (1, 2, 2, 2, 1)
-SIGN_ON_SCALAR = (4,)
+SIGN_ON_SCALAR = ((3, 1), (4, 0), (4, 1))
 W4 = P * 4
 S3 = 1.0 / math.sqrt(3.0)
 KNOT = (-0.6, -0.2, 0.2, 0.6)
+ONE_BY_MATMUL = (1,)
+SPLIT_ON_SCALAR = ((3, 1, 1),)
 RS = (1, 3, 0, 2)
 PSI_ON_PE = ((0, 1), (1, 1), (1, 0), (2, 1), (2, 0), (3, 1), (4, 1))
 PLANE = (1, 3, 5, 7, 0, 2, 4, 6)
@@ -45,8 +47,12 @@ def tile_kanlayer_kernel(tc, x, base_weight, spline_weight, out):
         nc.gpsimd.tensor_scalar(out=nident[:], in0=ident[:], scalar1=-1.0, scalar2=0.0, op0=ALU.mult, op1=ALU.add)
         minus = keep.tile([P, P], F32)
         nc.gpsimd.memset(minus[:], -1.0)
+        minus_part = keep.tile([P, P], BF16)
+        nc.gpsimd.memset(minus_part[:], -1.0 / P)
+        ones = keep.tile([P, W4], BF16)
+        nc.gpsimd.memset(ones[:], 1.0)
 
-        x_raw = keep.tile([P, B // P, I], BF16)
+        x_raw = half.tile([P, B // P, I], BF16, name="x_raw", tag="cc", bufs=2)
         x_rows = x.rearrange("(n p) i -> p n i", p=P)
         bw_raw = keep.tile([P, O // P, I], BF16)
         sw_raw = [keep.tile([P, I * L], BF16, name="sw_raw%d" % m) for m in range(O // P)]
@@ -123,10 +129,10 @@ def tile_kanlayer_kernel(tc, x, base_weight, spline_weight, out):
         def xc(c):
             return flat(xg[:, first[c] : first[c] + CHUNKS[c], :])
 
-        def a_wave(c, w, bank=None):
+        def a_fold(c, w, bank=None):
             n = CHUNKS[c] * W4
             z = wave.tile([P, n], F32, name="z%d" % w)
-            q = wave.tile([P, n], F32, name="q%d" % w)
+            zs[(c, w)] = z
             if bank is None:
                 nc.scalar.activation(out=z[:], in_=xc(c), func=ACT.Abs, bias=-0.5 - w, scale=2.5)
             else:
@@ -135,28 +141,45 @@ def tile_kanlayer_kernel(tc, x, base_weight, spline_weight, out):
                     in_=bank[:, 0].bitcast(BF16).rearrange("p u (b e) -> p b u e", e=2),
                     func=ACT.Abs, bias=-0.5 - w, scale=2.5,
                 )
-            nc.scalar.activation(out=z[:], in_=z[:], func=ACT.Abs, bias=-2.0, scale=1.0)
-            nc.scalar.activation(out=q[:], in_=z[:], func=ACT.Square, bias=-S3, scale=S3)
-            zs[(c, w)] = z
+
+        def a_fold2(c, w):
+            nc.scalar.activation(out=zs[(c, w)][:], in_=zs[(c, w)][:], func=ACT.Abs, bias=-2.0, scale=1.0)
+
+        def a_square(c, w):
+            q = wave.tile([P, CHUNKS[c] * W4], F32, name="q%d" % w)
             qs[(c, w)] = q
+            nc.scalar.activation(out=q[:], in_=zs[(c, w)][:], func=ACT.Square, bias=-S3, scale=S3)
+
+        def a_wave(c, w):
+            a_fold(c, w)
+            a_fold2(c, w)
+            a_square(c, w)
+
+        def a_waves(c, bank=None):
+            for w in (1, 0):
+                a_fold(c, w, bank)
+            for w in (1, 0):
+                a_fold2(c, w)
+            for w in (1, 0):
+                a_square(c, w)
 
         def d_xq(c):
             sl = slice(first[c], first[c] + CHUNKS[c])
             quantise(xc(c), flat(x_codes[:, sl, :]), flat(x_scales[:, sl, :]))
 
-        def gate(c):
-            n = CHUNKS[c] * W4
-            g = half.tile([P, 4, n], BF16, name="gate", bufs=2)
-            for i, r in enumerate(RS):
-                if c in SIGN_ON_SCALAR:
+        def gate(c, which=range(4)):
+            if c not in gates:
+                gates[c] = half.tile([P, 4, CHUNKS[c] * W4], BF16, name="gate", bufs=2)
+            for i in which:
+                r = RS[i]
+                if (c, i // 2) in SIGN_ON_SCALAR:
                     s = -1.0 if r < 2 else 1.0
-                    nc.scalar.activation(out=g[:, i, :], in_=xc(c), func=ACT.Sign, bias=-s * KNOT[r], scale=s)
+                    nc.scalar.activation(out=gates[c][:, i, :], in_=xc(c), func=ACT.Sign, bias=-s * KNOT[r], scale=s)
                 else:
                     nc.vector.tensor_scalar(
-                        out=g[:, i, :], in0=xc(c), scalar1=KNOT[r], scalar2=0.5,
+                        out=gates[c][:, i, :], in0=xc(c), scalar1=KNOT[r], scalar2=0.5,
                         op0=(ALU.is_lt if r < 2 else ALU.is_ge), op1=ALU.subtract,
                     )
-            gates[c] = g
 
         def d_cube(c, w):
             z, q = zs[(c, w)], qs[(c, w)]
@@ -177,10 +200,13 @@ def tile_kanlayer_kernel(tc, x, base_weight, spline_weight, out):
             sl = slice(n * W4, (n + 1) * W4)
             bank = psum.tile([P, W4], F32, name="psi", tag="bank")
             nc.tensor.matmul(bank[:], lhsT=ident[:], rhs=zs[(c, w)][:, sl], start=True, stop=False)
-            for h in range(4):
-                nc.tensor.matmul(
-                    bank[:, h * P : (h + 1) * P], lhsT=minus[:], rhs=ident[:], start=False, stop=False, is_transpose=True
-                )
+            if c in ONE_BY_MATMUL:
+                nc.tensor.matmul(bank[:], lhsT=minus_part[:], rhs=ones[:], start=False, stop=False)
+            else:
+                for h in range(4):
+                    nc.tensor.matmul(
+                        bank[:, h * P : (h + 1) * P], lhsT=minus[:], rhs=ident[:], start=False, stop=False, is_transpose=True
+                    )
             nc.tensor.matmul(bank[:], lhsT=nident[:], rhs=qs[(c, w)][:, sl], start=False, stop=True)
             psis[(c, n, w)] = bank
 
@@ -189,15 +215,15 @@ def tile_kanlayer_kernel(tc, x, base_weight, spline_weight, out):
             nc.scalar.activation(out=k[:], in_=qs[(c, w)][:], func=ACT.Abs, scale=0.5)
             ks[(c, w)] = k
 
-        def d_c1(c, w):
+        def d_c1(c, w, lows=(True, False)):
             if c not in ccs:
-                ccs[c] = half.tile([P, 4, CHUNKS[c] * W4], BF16, name="cc")
+                ccs[c] = half.tile([P, 4, CHUNKS[c] * W4], BF16, name="cc", tag="cc", bufs=2)
             n = CHUNKS[c]
             parts = [(m, slice(m * W4, (m + 1) * W4)) for m in range(n)] if (c, 0, w) in psis else [(None, slice(0, n * W4))]
             for m, sl in parts:
                 psi = zs[(c, w)][:, sl] if m is None else psis[(c, m, w)][:]
                 for i, r in enumerate(RS):
-                    if r % 2 == w:
+                    if r % 2 == w and (r < 2) in lows:
                         nc.vector.scalar_tensor_tensor(
                             out=ccs[c][:, i, sl], in0=psi, scalar=0.0, in1=ks[(c, 1 - w)][:, sl],
                             op0=(ALU.max if r < 2 else ALU.min), op1=(ALU.add if r < 2 else ALU.subtract),
@@ -212,11 +238,13 @@ def tile_kanlayer_kernel(tc, x, base_weight, spline_weight, out):
         def d_split(c, h, v):
             if c not in plane:
                 plane[c] = half.tile([P, L, CHUNKS[c] * W4], BF16, align_bytes=64, name="planes")
-            s = 1.0 if c in SIGN_ON_SCALAR else 2.0
-            nc.vector.tensor_scalar(
-                out=flat(plane[c][:, 4 * h + 2 * v : 4 * h + 2 * v + 2, :]), in0=flat(ccs[c][:, 2 * h : 2 * h + 2, :]),
-                scalar1=(s if v == 0 else -s), scalar2=0.0, op0=ALU.mult, op1=ALU.max,
-            )
+            s = 1.0 if (c, h) in SIGN_ON_SCALAR else 2.0
+            s = s if v == 0 else -s
+            dst, f = flat(plane[c][:, 4 * h + 2 * v : 4 * h + 2 * v + 2, :]), flat(ccs[c][:, 2 * h : 2 * h + 2, :])
+            if (c, h, v) in SPLIT_ON_SCALAR:
+                nc.scalar.activation(out=dst, in_=f, func=ACT.Relu, scale=s)
+            else:
+                nc.vector.tensor_scalar(out=dst, in0=f, scalar1=s, scalar2=0.0, op0=ALU.mult, op1=ALU.max)
 
         def d_pack(c, lo, hi):
             sl = slice(lo, hi)
@@ -287,8 +315,7 @@ def tile_kanlayer_kernel(tc, x, base_weight, spline_weight, out):
         turn_pe("xs", xw, 0, 1)
         turn_pe("xv", xw, 0, 1)
         turn_out(nc.vector.tensor_copy, "xv", xg, 0, 1)
-        a_wave(0, 1, banks["xs"])
-        a_wave(0, 0)
+        a_waves(0, banks["xs"])
         d_xq(0)
         gate(0)
         turn_pe("x1", xw, 1, 2)
@@ -311,8 +338,8 @@ def tile_kanlayer_kernel(tc, x, base_weight, spline_weight, out):
         d_xq(1)
         a_wave(1, 1)
         d_c1(0, 0)
-        d_c1(0, 1)
         gate(1)
+        d_c1(0, 1)
         d_mult(0, 1)
         a_wave(1, 0)
         d_cube(1, 1)
@@ -332,11 +359,12 @@ def tile_kanlayer_kernel(tc, x, base_weight, spline_weight, out):
         a_k(1, 0)
         a_wave(2, 1)
         a_wave(2, 0)
-        gate(2)
+        gate(2, (0, 1))
         d_xq(2)
-        d_c1(1, 1)
         d_xq(3)
         d_pack(0, 0, 4)
+        d_c1(1, 1)
+        gate(2, (2, 3))
         quantise(flat(bwg[:]), bw_codes[:], bw_scales[:])
         d_c1(1, 0)
         d_cube(2, 1)
@@ -371,60 +399,65 @@ def tile_kanlayer_kernel(tc, x, base_weight, spline_weight, out):
         a_k(3, 0)
         w_job(7)
         c2b(2)
-        d_psi(3, 0)
-        gate(3)
-        for k in range(8, 12):
-            w_job(k)
         w_q(1)
-        for k in range(12, 14):
+        d_psi(3, 0)
+        gate(3, (0, 1))
+        for k in range(8, 12):
             w_job(k)
         passes(0, (2, 3))
         passes(1, (2, 3))
+        for k in range(12, 14):
+            w_job(k)
         d_xq(4)
-        w_q(2)
         for k in range(14, 16):
             w_job(k)
-        a_wave(4, 1)
-        a_wave(4, 0)
+        a_waves(4)
         d_c1(3, 0)
+        w_q(2)
         d_c1(3, 1)
         passes(0, (4, 5))
         passes(1, (4, 5))
         passes(2, (-1, 0, 1, 2, 3, 4, 5))
+        gate(3, (2, 3))
         d_mult(3, 0)
         w_q(3)
+        d_split(3, 0, 0)
         d_cube(4, 1)
         make_psi(4, 1)
         a_k(4, 1)
-        d_split(3, 0, 0)
         d_split(3, 0, 1)
         d_cube(4, 0)
         a_k(4, 0)
-        make_psi(4, 0)
+        d_pack(3, 0, 4)
         d_mult(3, 1)
-        gate(4)
         for c in range(3):
             passes(c, (6, 7))
-        for t in range(5):
-            finish(t)
-        d_pack(3, 0, 4)
-        d_split(3, 1, 0)
         d_split(3, 1, 1)
+        d_split(3, 1, 0)
+        gate(4)
+        for t in range(3):
+            finish(t)
         d_psi(4, 0)
         d_c1(4, 1)
+        d_c1(4, 0, (True,))
         d_pack(3, 4, 8)
-        d_c1(4, 0)
         d_mult(4, 0)
-        d_mult(4, 1)
+        d_c1(4, 0, (False,))
+        passes(3, (-1,) + PLANE[0:4])
+        passes(3, PLANE[4:8])
+        finish(3)
+        finish(4)
         d_split(4, 0, 0)
         d_split(4, 0, 1)
-        d_split(4, 1, 0)
+        d_mult(4, 1)
         d_pack(4, 0, 4)
-        passes(3, (-1,) + PLANE)
         finish(5)
         finish(6)
         for half in range(2):
-            passes(4, (-1,) + PLANE[0:4], half)
+            passes(4, (-1,), half)
+        for half in range(2):
+            passes(4, PLANE[0:4], half)
+        d_split(4, 1, 0)
         d_split(4, 1, 1)
         d_pack(4, 4, 6)
         for half in range(2):

@@ -21,10 +21,10 @@ SIGN_ON_SCALAR = ((3, 1), (4, 0), (4, 1))
 W4 = P * 4
 S3 = 1.0 / math.sqrt(3.0)
 KNOT = (-0.6, -0.2, 0.2, 0.6)
-ONE_BY_MATMUL = (1,)
+ONE_BY_MATMUL = ((1, 1), (1, 0), (3, 1))
 SPLIT_ON_SCALAR = ((3, 1, 1),)
 RS = (1, 3, 0, 2)
-PSI_ON_PE = ((0, 1), (1, 1), (1, 0), (2, 1), (2, 0), (3, 1), (4, 1))
+PSI_ON_PE = ((0, 1, 0), (1, 1, 0), (1, 1, 1), (1, 0, 0), (1, 0, 1), (2, 1, 0), (2, 1, 1), (3, 1, 0), (3, 1, 1), (4, 1, 0), (2, 0, 1))
 PLANE = (1, 3, 5, 7, 0, 2, 4, 6)
 
 
@@ -187,20 +187,28 @@ def tile_kanlayer_kernel(tc, x, base_weight, spline_weight, out):
 
         psis = {}
 
-        def make_psi(c, w):
-            if (c, w) in PSI_ON_PE:
-                for n in range(CHUNKS[c]):
+        def make_psi(c, w, tiles=None):
+            for n in tiles or range(CHUNKS[c]):
+                if (c, w, n) in PSI_ON_PE:
                     pe_psi(c, n, w)
 
         def d_psi(c, w):
-            z, q = zs[(c, w)], qs[(c, w)]
-            nc.vector.scalar_tensor_tensor(out=z[:], in0=z[:], scalar=1.0, in1=q[:], op0=ALU.subtract, op1=ALU.subtract)
+            for n in range(CHUNKS[c]):
+                if (c, w, n) not in PSI_ON_PE:
+                    lo = n * W4
+                    hi = lo + W4 if (c, w, 0) in PSI_ON_PE or (c, w, 1) in PSI_ON_PE else CHUNKS[c] * W4
+                    if n > 0 and hi > lo + W4 or lo + W4 > hi:
+                        continue
+                    z, q = zs[(c, w)][:, lo:hi], qs[(c, w)][:, lo:hi]
+                    nc.vector.scalar_tensor_tensor(out=z, in0=z, scalar=1.0, in1=q, op0=ALU.subtract, op1=ALU.subtract)
+                    if hi > lo + W4:
+                        break
 
         def pe_psi(c, n, w):
             sl = slice(n * W4, (n + 1) * W4)
             bank = psum.tile([P, W4], F32, name="psi", tag="bank")
             nc.tensor.matmul(bank[:], lhsT=ident[:], rhs=zs[(c, w)][:, sl], start=True, stop=False)
-            if c in ONE_BY_MATMUL:
+            if (c, w) in ONE_BY_MATMUL:
                 nc.tensor.matmul(bank[:], lhsT=minus_part[:], rhs=ones[:], start=False, stop=False)
             else:
                 for h in range(4):
@@ -219,9 +227,10 @@ def tile_kanlayer_kernel(tc, x, base_weight, spline_weight, out):
             if c not in ccs:
                 ccs[c] = half.tile([P, 4, CHUNKS[c] * W4], BF16, name="cc", tag="cc", bufs=2)
             n = CHUNKS[c]
-            parts = [(m, slice(m * W4, (m + 1) * W4)) for m in range(n)] if (c, 0, w) in psis else [(None, slice(0, n * W4))]
+            split_up = any((c, m, w) in psis for m in range(n))
+            parts = [(m, slice(m * W4, (m + 1) * W4)) for m in range(n)] if split_up else [(None, slice(0, n * W4))]
             for m, sl in parts:
-                psi = zs[(c, w)][:, sl] if m is None else psis[(c, m, w)][:]
+                psi = psis[(c, m, w)][:] if (c, m, w) in psis else zs[(c, w)][:, sl]
                 for i, r in enumerate(RS):
                     if r % 2 == w and (r < 2) in lows:
                         nc.vector.scalar_tensor_tensor(
@@ -265,8 +274,8 @@ def tile_kanlayer_kernel(tc, x, base_weight, spline_weight, out):
         accs = {}
         count = {}
 
-        def passes(c, which, half=None):
-            for n in range(CHUNKS[c]):
+        def passes(c, which, half=None, tiles=None):
+            for n in tiles or range(CHUNKS[c]):
                 t = first[c] + n
                 cols = slice(n * P, (n + 1) * P)
                 key = t if half is None else (t, half)
@@ -327,6 +336,7 @@ def tile_kanlayer_kernel(tc, x, base_weight, spline_weight, out):
         d_cube(0, 1)
         make_psi(0, 1)
         turn_out(nc.vector.tensor_copy, "x4", xg, 4, 6)
+        a_fold(1, 1)
         a_k(0, 1)
         d_cube(0, 0)
         turn_out(nc.vector.tensor_copy, "x6", xg, 6, 8)
@@ -336,7 +346,8 @@ def tile_kanlayer_kernel(tc, x, base_weight, spline_weight, out):
         d_psi(0, 0)
         a_k(0, 0)
         d_xq(1)
-        a_wave(1, 1)
+        a_fold2(1, 1)
+        a_square(1, 1)
         d_c1(0, 0)
         gate(1)
         d_c1(0, 1)
@@ -357,8 +368,7 @@ def tile_kanlayer_kernel(tc, x, base_weight, spline_weight, out):
         w_ahead(3)
         make_psi(1, 0)
         a_k(1, 0)
-        a_wave(2, 1)
-        a_wave(2, 0)
+        a_waves(2)
         gate(2, (0, 1))
         d_xq(2)
         d_xq(3)
@@ -369,20 +379,23 @@ def tile_kanlayer_kernel(tc, x, base_weight, spline_weight, out):
         d_c1(1, 0)
         d_cube(2, 1)
         make_psi(2, 1)
+        w_job(0)
         a_k(2, 1)
         c2a(1)
-        w_job(0)
-        d_cube(2, 0)
-        w_ahead(4)
-        make_psi(2, 0)
         w_job(1)
-        a_k(2, 0)
-        c2b(1)
+        d_cube(2, 0)
+        w_ahead(5)
+        make_psi(2, 0)
         w_job(2)
+        a_k(2, 0)
+        d_split(1, 1, 0)
+        d_psi(2, 0)
+        d_split(1, 1, 1)
+        d_pack(1, 0, 4)
+        d_pack(1, 4, 8)
         w_job(3)
         w_q(0)
-        a_wave(3, 1)
-        a_wave(3, 0)
+        a_waves(3)
         d_c1(2, 1)
         d_c1(2, 0)
         passes(0, (-1, 0, 1))
@@ -396,8 +409,8 @@ def tile_kanlayer_kernel(tc, x, base_weight, spline_weight, out):
         w_job(5)
         w_job(6)
         d_cube(3, 0)
-        a_k(3, 0)
         w_job(7)
+        a_k(3, 0)
         c2b(2)
         w_q(1)
         d_psi(3, 0)
@@ -422,22 +435,23 @@ def tile_kanlayer_kernel(tc, x, base_weight, spline_weight, out):
         d_mult(3, 0)
         w_q(3)
         d_split(3, 0, 0)
+        d_split(3, 0, 1)
+        for c in range(2):
+            passes(c, (6, 7))
         d_cube(4, 1)
         make_psi(4, 1)
+        passes(2, (6, 7))
         a_k(4, 1)
-        d_split(3, 0, 1)
+        d_pack(3, 0, 4)
         d_cube(4, 0)
         a_k(4, 0)
-        d_pack(3, 0, 4)
         d_mult(3, 1)
-        for c in range(3):
-            passes(c, (6, 7))
+        d_psi(4, 0)
         d_split(3, 1, 1)
         d_split(3, 1, 0)
         gate(4)
         for t in range(3):
             finish(t)
-        d_psi(4, 0)
         d_c1(4, 1)
         d_c1(4, 0, (True,))
         d_pack(3, 4, 8)

@@ -22,7 +22,7 @@ W4 = P * 4
 S3 = 1.0 / math.sqrt(3.0)
 KNOT = (-0.6, -0.2, 0.2, 0.6)
 ONE_BY_MATMUL = ((1, 1), (1, 0), (3, 1))
-SPLIT_ON_SCALAR = ((3, 1, 1),)
+SPLIT_ON_SCALAR = ((3, 1, 1), (0, 0, 1))
 RS = (1, 3, 0, 2)
 PSI_ON_PE = ((0, 1, 0), (1, 1, 0), (1, 1, 1), (1, 0, 0), (1, 0, 1), (2, 1, 0), (2, 1, 1), (3, 1, 0), (3, 1, 1), (4, 1, 0), (2, 0, 1))
 PLANE = (1, 3, 5, 7, 0, 2, 4, 6)
@@ -240,9 +240,10 @@ def tile_kanlayer_kernel(tc, x, base_weight, spline_weight, out):
 
         plane = {}
 
-        def d_mult(c, h):
-            f = flat(ccs[c][:, 2 * h : 2 * h + 2, :])
-            nc.vector.tensor_tensor(out=f, in0=f, in1=flat(gates[c][:, 2 * h : 2 * h + 2, :]), op=ALU.mult)
+        def d_mult(c, h=None):
+            sl = slice(0, 4) if h is None else slice(2 * h, 2 * h + 2)
+            f = flat(ccs[c][:, sl, :])
+            nc.vector.tensor_tensor(out=f, in0=f, in1=flat(gates[c][:, sl, :]), op=ALU.mult)
 
         def d_split(c, h, v):
             if c not in plane:
@@ -305,10 +306,10 @@ def tile_kanlayer_kernel(tc, x, base_weight, spline_weight, out):
             nc.scalar.copy(out=r[:], in_=accs[t][:])
             nc.sync.dma_start(out=out[t * P : (t + 1) * P, :], in_=r[:])
 
-        def finish_half(t, half, copy):
+        def finish_half(t, half, copy, queue):
             r = res.tile([P, O // 2], F32, name="rh", bufs=2)
             copy(out=r[:], in_=accs[(t, half)][:, 0 : O // 2])
-            nc.sync.dma_start(out=out[t * P : (t + 1) * P, half * (O // 2) : (half + 1) * (O // 2)], in_=r[:])
+            queue.dma_start(out=out[t * P : (t + 1) * P, half * (O // 2) : (half + 1) * (O // 2)], in_=r[:])
 
         ahead = [0]
 
@@ -381,9 +382,11 @@ def tile_kanlayer_kernel(tc, x, base_weight, spline_weight, out):
         make_psi(2, 1)
         w_job(0)
         a_k(2, 1)
-        c2a(1)
+        d_mult(1)
         w_job(1)
         d_cube(2, 0)
+        d_split(1, 0, 0)
+        d_split(1, 0, 1)
         w_ahead(5)
         make_psi(2, 0)
         w_job(2)
@@ -402,13 +405,16 @@ def tile_kanlayer_kernel(tc, x, base_weight, spline_weight, out):
         passes(1, (-1, 0, 1))
         d_cube(3, 1)
         w_ahead(7)
-        make_psi(3, 1)
+        make_psi(3, 1, (0,))
         w_job(4)
         a_k(3, 1)
-        c2a(2)
+        d_mult(2)
         w_job(5)
+        make_psi(3, 1, (1,))
         w_job(6)
         d_cube(3, 0)
+        d_split(2, 0, 0)
+        d_split(2, 0, 1)
         w_job(7)
         a_k(3, 0)
         c2b(2)
@@ -424,13 +430,14 @@ def tile_kanlayer_kernel(tc, x, base_weight, spline_weight, out):
         d_xq(4)
         for k in range(14, 16):
             w_job(k)
+        passes(2, (-1, 0, 1, 2, 3))
         a_waves(4)
         d_c1(3, 0)
         w_q(2)
         d_c1(3, 1)
         passes(0, (4, 5))
         passes(1, (4, 5))
-        passes(2, (-1, 0, 1, 2, 3, 4, 5))
+        passes(2, (4, 5))
         gate(3, (2, 3))
         d_mult(3, 0)
         w_q(3)
@@ -479,5 +486,5 @@ def tile_kanlayer_kernel(tc, x, base_weight, spline_weight, out):
         d_pack(4, 6, 8)
         for half in range(2):
             passes(4, PLANE[6:8], half)
-        finish_half(7, 0, nc.scalar.copy)
-        finish_half(7, 1, nc.vector.tensor_copy)
+        finish_half(7, 0, nc.scalar.copy, nc.sync)
+        finish_half(7, 1, nc.vector.tensor_copy, nc.scalar)

@@ -21,10 +21,10 @@ SIGN_ON_SCALAR = ((3, 1), (4, 0), (4, 1))
 W4 = P * 4
 S3 = 1.0 / math.sqrt(3.0)
 KNOT = (-0.6, -0.2, 0.2, 0.6)
-ONE_BY_MATMUL = ((1, 1), (1, 0), (3, 1))
-SPLIT_ON_SCALAR = ((3, 1, 1), (0, 0, 1))
+ONE_BY_MATMUL = ((0, 1), (1, 1), (1, 0), (3, 1))
+SPLIT_ON_SCALAR = {(3, 1, 1): 2, (0, 0, 1): 2, (1, 1, 1): 1}
 RS = (1, 3, 0, 2)
-PSI_ON_PE = ((0, 1, 0), (1, 1, 0), (1, 1, 1), (1, 0, 0), (1, 0, 1), (2, 1, 0), (2, 1, 1), (3, 1, 0), (3, 1, 1), (4, 1, 0), (2, 0, 1))
+PSI_ON_PE = ((0, 1, 0), (1, 1, 0), (1, 1, 1), (2, 1, 0), (2, 1, 1), (3, 1, 0), (3, 1, 1), (4, 1, 0), (1, 0, 0), (2, 0, 1))
 PLANE = (1, 3, 5, 7, 0, 2, 4, 6)
 
 
@@ -251,10 +251,12 @@ def tile_kanlayer_kernel(tc, x, base_weight, spline_weight, out):
             s = 1.0 if (c, h) in SIGN_ON_SCALAR else 2.0
             s = s if v == 0 else -s
             dst, f = flat(plane[c][:, 4 * h + 2 * v : 4 * h + 2 * v + 2, :]), flat(ccs[c][:, 2 * h : 2 * h + 2, :])
-            if (c, h, v) in SPLIT_ON_SCALAR:
-                nc.scalar.activation(out=dst, in_=f, func=ACT.Relu, scale=s)
-            else:
-                nc.vector.tensor_scalar(out=dst, in0=f, scalar1=s, scalar2=0.0, op0=ALU.mult, op1=ALU.max)
+            n = CHUNKS[c] * W4
+            cut = SPLIT_ON_SCALAR.get((c, h, v), 0) * n
+            if cut > 0:
+                nc.scalar.activation(out=dst[:, 0:cut], in_=f[:, 0:cut], func=ACT.Relu, scale=s)
+            if cut < 2 * n:
+                nc.vector.tensor_scalar(out=dst[:, cut:], in0=f[:, cut:], scalar1=s, scalar2=0.0, op0=ALU.mult, op1=ALU.max)
 
         def d_pack(c, lo, hi):
             sl = slice(lo, hi)
@@ -373,6 +375,7 @@ def tile_kanlayer_kernel(tc, x, base_weight, spline_weight, out):
         gate(2, (0, 1))
         d_xq(2)
         d_xq(3)
+        d_psi(1, 0)
         d_pack(0, 0, 4)
         d_c1(1, 1)
         gate(2, (2, 3))
@@ -389,11 +392,11 @@ def tile_kanlayer_kernel(tc, x, base_weight, spline_weight, out):
         d_split(1, 0, 1)
         w_ahead(5)
         make_psi(2, 0)
+        d_split(1, 1, 1)
         w_job(2)
         a_k(2, 0)
         d_split(1, 1, 0)
         d_psi(2, 0)
-        d_split(1, 1, 1)
         d_pack(1, 0, 4)
         d_pack(1, 4, 8)
         w_job(3)

@@ -21,10 +21,10 @@ SIGN_ON_SCALAR = ((3, 1), (4, 0), (4, 1))
 W4 = P * 4
 S3 = 1.0 / math.sqrt(3.0)
 KNOT = (-0.6, -0.2, 0.2, 0.6)
-ONE_BY_MATMUL = ((0, 1), (1, 1), (1, 0), (3, 1))
+ONE_BY_MATMUL = ((1, 1), (1, 0), (3, 1))
 SPLIT_ON_SCALAR = {(3, 1, 1): 2, (0, 0, 1): 2, (1, 1, 1): 1}
 RS = (1, 3, 0, 2)
-PSI_ON_PE = ((0, 1, 0), (1, 1, 0), (1, 1, 1), (2, 1, 0), (2, 1, 1), (3, 1, 0), (3, 1, 1), (4, 1, 0), (1, 0, 0), (2, 0, 1))
+PSI_ON_PE = ((0, 1, 0), (1, 1, 0), (1, 1, 1), (2, 1, 0), (2, 1, 1), (2, 0, 0), (2, 0, 1), (3, 1, 0), (3, 1, 1), (4, 1, 0), (1, 0, 0))
 PLANE = (1, 3, 5, 7, 0, 2, 4, 6)
 
 
@@ -396,7 +396,6 @@ def tile_kanlayer_kernel(tc, x, base_weight, spline_weight, out):
         w_job(2)
         a_k(2, 0)
         d_split(1, 1, 0)
-        d_psi(2, 0)
         d_pack(1, 0, 4)
         d_pack(1, 4, 8)
         w_job(3)

import math
from contextlib import ExitStack

import concourse.mybir as mybir
from concourse.masks import make_identity

F32 = mybir.dt.float32
BF16 = mybir.dt.bfloat16
U32 = mybir.dt.uint32
U8 = mybir.dt.uint8
FP8X4 = mybir.dt.float8_e4m3fn_x4
ACT = mybir.ActivationFunctionType
ALU = mybir.AluOpType

P = 128
B, I, O, L = 1024, 512, 512, 8
FLOPS = 2 * B * O * (I + I * L)

CHUNKS = (1, 2, 2, 2, 1)
SIGN_ON_SCALAR = ((3, 1), (4, 0), (4, 1))
W4 = P * 4
S3 = 1.0 / math.sqrt(3.0)
KNOT = (-0.6, -0.2, 0.2, 0.6)
ONE_BY_MATMUL = ((1, 1), (1, 0), (3, 1))
SPLIT_ON_SCALAR = {(3, 1, 1): 2, (0, 0, 1): 2, (1, 1, 1): 1}
RS = (1, 3, 0, 2)
PSI_ON_PE = ((0, 1, 0), (1, 1, 0), (1, 1, 1), (2, 1, 0), (2, 1, 1), (2, 0, 0), (2, 0, 1), (3, 1, 0), (3, 1, 1), (4, 1, 0), (1, 0, 0))
PLANE = (1, 3, 5, 7, 0, 2, 4, 6)


def tile_kanlayer_kernel(tc, x, base_weight, spline_weight, out):
    nc = tc.nc
    nch = len(CHUNKS)
    first = [sum(CHUNKS[:c]) for c in range(nch)]
    with ExitStack() as ctx:
        keep = ctx.enter_context(tc.tile_pool(name="keep", bufs=1))
        wave = ctx.enter_context(tc.tile_pool(name="wave", bufs=2))
        half = ctx.enter_context(tc.tile_pool(name="half", bufs=1))
        grp = ctx.enter_context(tc.tile_pool(name="grp", bufs=2))
        res = ctx.enter_context(tc.tile_pool(name="res", bufs=7))
        psum = ctx.enter_context(tc.psum_pool(name="psum", bufs=8))
        ctx.enter_context(tc.manual_schedule())

        ident = keep.tile([P, P], F32)
        make_identity(nc, ident[:])
        nident = keep.tile([P, P], F32)
        nc.gpsimd.tensor_scalar(out=nident[:], in0=ident[:], scalar1=-1.0, scalar2=0.0, op0=ALU.mult, op1=ALU.add)
        minus = keep.tile([P, P], F32)
        nc.gpsimd.memset(minus[:], -1.0)
        minus_part = keep.tile([P, P], BF16)
        nc.gpsimd.memset(minus_part[:], -1.0 / P)
        ones = keep.tile([P, W4], BF16)
        nc.gpsimd.memset(ones[:], 1.0)

        x_raw = half.tile([P, B // P, I], BF16, name="x_raw", tag="cc", bufs=2)
        x_rows = x.rearrange("(n p) i -> p n i", p=P)
        bw_raw = keep.tile([P, O // P, I], BF16)
        sw_raw = [keep.tile([P, I * L], BF16, name="sw_raw%d" % m) for m in range(O // P)]
        sw_rows = spline_weight.rearrange("(m p) i l -> m p (i l)", p=P)
        for lo, hi in ((0, 1), (1, 3), (3, 8)):
            nc.sync.dma_start(out=x_raw[:, lo:hi, :], in_=x_rows[:, lo:hi, :])
        nc.sync.dma_start(out=bw_raw[:], in_=base_weight.rearrange("(m p) i -> p m i", p=P))
        for m in range(O // P):
            nc.sync.dma_start(out=sw_raw[m][:], in_=sw_rows[m])

        xg = keep.tile([P, B // P, W4], BF16, align_bytes=64)
        x_codes = keep.tile([P, B // P, P], U32, align_bytes=64)
        x_scales = keep.tile([P, B // P, P], U8, align_bytes=64)
        bwg = keep.tile([P, O // P, W4], BF16, align_bytes=64)
        bw_codes = keep.tile([P, O], U32, align_bytes=64)
        bw_scales = keep.tile([P, O], U8, align_bytes=64)
        w_codes = keep.tile([P, L, O], U32, align_bytes=64)
        w_scales = keep.tile([P, L, O], U8, align_bytes=64)
        b_codes = [keep.tile([P, L, CHUNKS[c] * P], U32, align_bytes=64, name="b_codes%d" % c) for c in range(nch)]
        b_scales = [keep.tile([P, L, CHUNKS[c] * P], U8, align_bytes=64, name="b_scales%d" % c) for c in range(nch)]

        xw = x_raw[:].bitcast(F32)
        bww = bw_raw[:].bitcast(F32)
        banks = {}

        def quantise(src, codes, scales):
            nc.vector.quantize_mx(out=codes.bitcast(FP8X4), scales=scales, in_=src)

        def flat(ap):
            return ap.rearrange("p a b -> p (a b)")

        def turn_pe(key, words, lo, hi):
            bank = psum.tile([P, 2, 2, P], F32, name="bank", tag="bank")
            for n in range(lo, hi):
                for u in range(2):
                    nc.tensor.transpose(bank[:, n - lo, u, :], words[:, n, u * P : (u + 1) * P], ident[:])
            banks[key] = bank

        def turn_out(copy, key, dst, lo, hi):
            copy(
                out=flat(dst[:, lo:hi, :]).bitcast(F32).rearrange("p (n b u) -> p n b u", n=hi - lo, u=2),
                in_=banks[key][:, 0 : hi - lo].rearrange("p n u b -> p n b u"),
            )

        groups = {}

        def w_pe(k):
            j, m = k // 4, k % 4
            words = sw_raw[m][:].bitcast(F32).rearrange("p (u q e j) -> p u e j q", u=2, q=P, e=2, j=4)
            bank = psum.tile([P, 4, P], F32, name="wbank", tag="bank")
            for u in range(2):
                for e in range(2):
                    nc.tensor.transpose(bank[:, 2 * u + e, :], words[:, u, e, j, :], ident[:])
            banks[("w", k)] = bank

        def w_act(k):
            j, m = k // 4, k % 4
            if m == 0:
                groups[j] = grp.tile([P, 2, O, 4], BF16, align_bytes=64, name="g")
            nc.scalar.copy(
                out=groups[j][:, :, m * P : (m + 1) * P, :],
                in_=banks[("w", k)][:].bitcast(BF16).rearrange("p t (o s) -> p s o t", s=2),
            )

        def w_q(j):
            quantise(
                groups[j][:].rearrange("p s o t -> p (s o t)"),
                flat(w_codes[:, 2 * j : 2 * j + 2, :]),
                flat(w_scales[:, 2 * j : 2 * j + 2, :]),
            )

        zs, qs, ks, gates, ccs = {}, {}, {}, {}, {}

        def xc(c):
            return flat(xg[:, first[c] : first[c] + CHUNKS[c], :])

        def a_fold(c, w, bank=None):
            n = CHUNKS[c] * W4
            z = wave.tile([P, n], F32, name="z%d" % w)
            zs[(c, w)] = z
            if bank is None:
                nc.scalar.activation(out=z[:], in_=xc(c), func=ACT.Abs, bias=-0.5 - w, scale=2.5)
            else:
                nc.scalar.activation(
                    out=z[:].rearrange("p (b u e) -> p b u e", u=2, e=2),
                    in_=bank[:, 0].bitcast(BF16).rearrange("p u (b e) -> p b u e", e=2),
                    func=ACT.Abs, bias=-0.5 - w, scale=2.5,
                )

        def a_fold2(c, w):
            nc.scalar.activation(out=zs[(c, w)][:], in_=zs[(c, w)][:], func=ACT.Abs, bias=-2.0, scale=1.0)

        def a_square(c, w):
            q = wave.tile([P, CHUNKS[c] * W4], F32, name="q%d" % w)
            qs[(c, w)] = q
            nc.scalar.activation(out=q[:], in_=zs[(c, w)][:], func=ACT.Square, bias=-S3, scale=S3)

        def a_wave(c, w):
            a_fold(c, w)
            a_fold2(c, w)
            a_square(c, w)

        def a_waves(c, bank=None):
            for w in (1, 0):
                a_fold(c, w, bank)
            for w in (1, 0):
                a_fold2(c, w)
            for w in (1, 0):
                a_square(c, w)

        def d_xq(c):
            sl = slice(first[c], first[c] + CHUNKS[c])
            quantise(xc(c), flat(x_codes[:, sl, :]), flat(x_scales[:, sl, :]))

        def gate(c, which=range(4)):
            if c not in gates:
                gates[c] = half.tile([P, 4, CHUNKS[c] * W4], BF16, name="gate", bufs=2)
            for i in which:
                r = RS[i]
                if (c, i // 2) in SIGN_ON_SCALAR:
                    s = -1.0 if r < 2 else 1.0
                    nc.scalar.activation(out=gates[c][:, i, :], in_=xc(c), func=ACT.Sign, bias=-s * KNOT[r], scale=s)
                else:
                    nc.vector.tensor_scalar(
                        out=gates[c][:, i, :], in0=xc(c), scalar1=KNOT[r], scalar2=0.5,
                        op0=(ALU.is_lt if r < 2 else ALU.is_ge), op1=ALU.subtract,
                    )

        def d_cube(c, w):
            z, q = zs[(c, w)], qs[(c, w)]
            nc.vector.scalar_tensor_tensor(out=q[:], in0=z[:], scalar=1.0, in1=q[:], op0=ALU.subtract, op1=ALU.mult)

        psis = {}

        def make_psi(c, w, tiles=None):
            for n in tiles or range(CHUNKS[c]):
                if (c, w, n) in PSI_ON_PE:
                    pe_psi(c, n, w)

        def d_psi(c, w):
            for n in range(CHUNKS[c]):
                if (c, w, n) not in PSI_ON_PE:
                    lo = n * W4
                    hi = lo + W4 if (c, w, 0) in PSI_ON_PE or (c, w, 1) in PSI_ON_PE else CHUNKS[c] * W4
                    if n > 0 and hi > lo + W4 or lo + W4 > hi:
                        continue
                    z, q = zs[(c, w)][:, lo:hi], qs[(c, w)][:, lo:hi]
                    nc.vector.scalar_tensor_tensor(out=z, in0=z, scalar=1.0, in1=q, op0=ALU.subtract, op1=ALU.subtract)
                    if hi > lo + W4:
                        break

        def pe_psi(c, n, w):
            sl = slice(n * W4, (n + 1) * W4)
            bank = psum.tile([P, W4], F32, name="psi", tag="bank")
            nc.tensor.matmul(bank[:], lhsT=ident[:], rhs=zs[(c, w)][:, sl], start=True, stop=False)
            if (c, w) in ONE_BY_MATMUL:
                nc.tensor.matmul(bank[:], lhsT=minus_part[:], rhs=ones[:], start=False, stop=False)
            else:
                for h in range(4):
                    nc.tensor.matmul(
                        bank[:, h * P : (h + 1) * P], lhsT=minus[:], rhs=ident[:], start=False, stop=False, is_transpose=True
                    )
            nc.tensor.matmul(bank[:], lhsT=nident[:], rhs=qs[(c, w)][:, sl], start=False, stop=True)
            psis[(c, n, w)] = bank

        def a_k(c, w):
            k = half.tile([P, CHUNKS[c] * W4], F32, name="k%d" % w)
            nc.scalar.activation(out=k[:], in_=qs[(c, w)][:], func=ACT.Abs, scale=0.5)
            ks[(c, w)] = k

        def d_c1(c, w, lows=(True, False)):
            if c not in ccs:
                ccs[c] = half.tile([P, 4, CHUNKS[c] * W4], BF16, name="cc", tag="cc", bufs=2)
            n = CHUNKS[c]
            split_up = any((c, m, w) in psis for m in range(n))
            parts = [(m, slice(m * W4, (m + 1) * W4)) for m in range(n)] if split_up else [(None, slice(0, n * W4))]
            for m, sl in parts:
                psi = psis[(c, m, w)][:] if (c, m, w) in psis else zs[(c, w)][:, sl]
                for i, r in enumerate(RS):
                    if r % 2 == w and (r < 2) in lows:
                        nc.vector.scalar_tensor_tensor(
                            out=ccs[c][:, i, sl], in0=psi, scalar=0.0, in1=ks[(c, 1 - w)][:, sl],
                            op0=(ALU.max if r < 2 else ALU.min), op1=(ALU.add if r < 2 else ALU.subtract),
                        )

        plane = {}

        def d_mult(c, h=None):
            sl = slice(0, 4) if h is None else slice(2 * h, 2 * h + 2)
            f = flat(ccs[c][:, sl, :])
            nc.vector.tensor_tensor(out=f, in0=f, in1=flat(gates[c][:, sl, :]), op=ALU.mult)

        def d_split(c, h, v):
            if c not in plane:
                plane[c] = half.tile([P, L, CHUNKS[c] * W4], BF16, align_bytes=64, name="planes")
            s = 1.0 if (c, h) in SIGN_ON_SCALAR else 2.0
            s = s if v == 0 else -s
            dst, f = flat(plane[c][:, 4 * h + 2 * v : 4 * h + 2 * v + 2, :]), flat(ccs[c][:, 2 * h : 2 * h + 2, :])
            n = CHUNKS[c] * W4
            cut = SPLIT_ON_SCALAR.get((c, h, v), 0) * n
            if cut > 0:
                nc.scalar.activation(out=dst[:, 0:cut], in_=f[:, 0:cut], func=ACT.Relu, scale=s)
            if cut < 2 * n:
                nc.vector.tensor_scalar(out=dst[:, cut:], in0=f[:, cut:], scalar1=s, scalar2=0.0, op0=ALU.mult, op1=ALU.max)

        def d_pack(c, lo, hi):
            sl = slice(lo, hi)
            quantise(flat(plane[c][:, sl, :]), flat(b_codes[c][:, sl, :]), flat(b_scales[c][:, sl, :]))

        def c2a(c):
            d_mult(c, 0)
            d_mult(c, 1)
            d_split(c, 0, 0)
            d_split(c, 0, 1)

        def c2b(c):
            d_split(c, 1, 0)
            d_split(c, 1, 1)
            d_pack(c, 0, 4)
            d_pack(c, 4, 8)

        accs = {}
        count = {}

        def passes(c, which, half=None, tiles=None):
            for n in tiles or range(CHUNKS[c]):
                t = first[c] + n
                cols = slice(n * P, (n + 1) * P)
                key = t if half is None else (t, half)
                oc = slice(0, O) if half is None else slice(half * (O // 2), (half + 1) * (O // 2))
                for l in which:
                    if key not in accs:
                        accs[key] = psum.tile([P, O], F32, name="acc", tag="bank")
                        count[key] = 0
                    count[key] += 1
                    acc = accs[key][:, 0 : oc.stop - oc.start]
                    if l < 0:
                        nc.tensor.matmul_mx(
                            out=acc, lhsT=x_codes[:, t, :].bitcast(FP8X4), lhsT_scale=x_scales[:, t, :],
                            rhs=bw_codes[:, oc].bitcast(FP8X4), rhs_scale=bw_scales[:, oc],
                            start=(count[key] == 1), stop=(count[key] == L + 1),
                        )
                    else:
                        i = PLANE.index(l)
                        nc.tensor.matmul_mx(
                            out=acc, lhsT=b_codes[c][:, i, cols].bitcast(FP8X4), lhsT_scale=b_scales[c][:, i, cols],
                            rhs=w_codes[:, l, oc].bitcast(FP8X4), rhs_scale=w_scales[:, l, oc],
                            start=(count[key] == 1), stop=(count[key] == L + 1),
                        )

        def finish(t):
            r = res.tile([P, O], F32, name="r")
            nc.scalar.copy(out=r[:], in_=accs[t][:])
            nc.sync.dma_start(out=out[t * P : (t + 1) * P, :], in_=r[:])

        def finish_half(t, half, copy, queue):
            r = res.tile([P, O // 2], F32, name="rh", bufs=2)
            copy(out=r[:], in_=accs[(t, half)][:, 0 : O // 2])
            queue.dma_start(out=out[t * P : (t + 1) * P, half * (O // 2) : (half + 1) * (O // 2)], in_=r[:])

        ahead = [0]

        def w_ahead(k):
            for j in range(ahead[0], min(k, 16)):
                w_pe(j)
                ahead[0] = j + 1

        def w_job(k):
            w_act(k)
            w_ahead(k + 3)

        turn_pe("xs", xw, 0, 1)
        turn_pe("xv", xw, 0, 1)
        turn_out(nc.vector.tensor_copy, "xv", xg, 0, 1)
        a_waves(0, banks["xs"])
        d_xq(0)
        gate(0)
        turn_pe("x1", xw, 1, 2)
        turn_out(nc.vector.tensor_copy, "x1", xg, 1, 2)
        turn_pe("x2", xw, 2, 4)
        turn_out(nc.vector.tensor_copy, "x2", xg, 2, 4)
        turn_pe("x4", xw, 4, 6)
        turn_pe("x6", xw, 6, 8)
        d_cube(0, 1)
        make_psi(0, 1)
        turn_out(nc.vector.tensor_copy, "x4", xg, 4, 6)
        a_fold(1, 1)
        a_k(0, 1)
        d_cube(0, 0)
        turn_out(nc.vector.tensor_copy, "x6", xg, 6, 8)
        turn_pe("b0", bww, 0, 2)
        turn_pe("b1", bww, 2, 4)
        w_ahead(2)
        d_psi(0, 0)
        a_k(0, 0)
        d_xq(1)
        a_fold2(1, 1)
        a_square(1, 1)
        d_c1(0, 0)
        gate(1)
        d_c1(0, 1)
        d_mult(0, 1)
        a_wave(1, 0)
        d_cube(1, 1)
        make_psi(1, 1)
        a_k(1, 1)
        turn_out(nc.scalar.copy, "b0", bwg, 0, 2)
        turn_out(nc.scalar.copy, "b1", bwg, 2, 4)
        d_mult(0, 0)
        d_split(0, 1, 0)
        d_split(0, 1, 1)
        d_split(0, 0, 0)
        d_split(0, 0, 1)
        d_pack(0, 4, 8)
        d_cube(1, 0)
        w_ahead(3)
        make_psi(1, 0)
        a_k(1, 0)
        a_waves(2)
        gate(2, (0, 1))
        d_xq(2)
        d_xq(3)
        d_psi(1, 0)
        d_pack(0, 0, 4)
        d_c1(1, 1)
        gate(2, (2, 3))
        quantise(flat(bwg[:]), bw_codes[:], bw_scales[:])
        d_c1(1, 0)
        d_cube(2, 1)
        make_psi(2, 1)
        w_job(0)
        a_k(2, 1)
        d_mult(1)
        w_job(1)
        d_cube(2, 0)
        d_split(1, 0, 0)
        d_split(1, 0, 1)
        w_ahead(5)
        make_psi(2, 0)
        d_split(1, 1, 1)
        w_job(2)
        a_k(2, 0)
        d_split(1, 1, 0)
        d_pack(1, 0, 4)
        d_pack(1, 4, 8)
        w_job(3)
        w_q(0)
        a_waves(3)
        d_c1(2, 1)
        d_c1(2, 0)
        passes(0, (-1, 0, 1))
        passes(1, (-1, 0, 1))
        d_cube(3, 1)
        w_ahead(7)
        make_psi(3, 1, (0,))
        w_job(4)
        a_k(3, 1)
        d_mult(2)
        w_job(5)
        make_psi(3, 1, (1,))
        w_job(6)
        d_cube(3, 0)
        d_split(2, 0, 0)
        d_split(2, 0, 1)
        w_job(7)
        a_k(3, 0)
        c2b(2)
        w_q(1)
        d_psi(3, 0)
        gate(3, (0, 1))
        for k in range(8, 12):
            w_job(k)
        passes(0, (2, 3))
        passes(1, (2, 3))
        for k in range(12, 14):
            w_job(k)
        d_xq(4)
        for k in range(14, 16):
            w_job(k)
        passes(2, (-1, 0, 1, 2, 3))
        a_waves(4)
        d_c1(3, 0)
        w_q(2)
        d_c1(3, 1)
        passes(0, (4, 5))
        passes(1, (4, 5))
        passes(2, (4, 5))
        gate(3, (2, 3))
        d_mult(3, 0)
        w_q(3)
        d_split(3, 0, 0)
        d_split(3, 0, 1)
        for c in range(2):
            passes(c, (6, 7))
        d_cube(4, 1)
        make_psi(4, 1)
        passes(2, (6, 7))
        a_k(4, 1)
        d_pack(3, 0, 4)
        d_cube(4, 0)
        a_k(4, 0)
        d_mult(3, 1)
        d_psi(4, 0)
        d_split(3, 1, 1)
        d_split(3, 1, 0)
        gate(4)
        for t in range(3):
            finish(t)
        d_c1(4, 1)
        d_c1(4, 0, (True,))
        d_pack(3, 4, 8)
        d_mult(4, 0)
        d_c1(4, 0, (False,))
        passes(3, (-1,) + PLANE[0:4])
        passes(3, PLANE[4:8])
        finish(3)
        finish(4)
        d_split(4, 0, 0)
        d_split(4, 0, 1)
        d_mult(4, 1)
        d_pack(4, 0, 4)
        finish(5)
        finish(6)
        for half in range(2):
            passes(4, (-1,), half)
        for half in range(2):
            passes(4, PLANE[0:4], half)
        d_split(4, 1, 0)
        d_split(4, 1, 1)
        d_pack(4, 4, 6)
        for half in range(2):
            passes(4, PLANE[4:6], half)
        d_pack(4, 6, 8)
        for half in range(2):
            passes(4, PLANE[6:8], half)
        finish_half(7, 0, nc.scalar.copy, nc.sync)
        finish_half(7, 1, nc.vector.tensor_copy, nc.scalar)
